import numpy as np
import ml_dtypes


def mxq(x, axis, fmt="e4m3"):
    dtype, down = {"e4m3": (ml_dtypes.float8_e4m3fn, 7), "e5m2": (ml_dtypes.float8_e5m2, 14)}[fmt]
    v = np.moveaxis(np.asarray(x, np.float32).astype(ml_dtypes.bfloat16).astype(np.float64), axis, -1)
    blocks = v.reshape(v.shape[:-1] + (-1, 32))
    amax = np.abs(blocks).max(-1, keepdims=True)
    byte = np.maximum(np.where(amax > 0, np.frexp(amax)[1] - 1 + 127, 0) - down, 1)
    scale = np.exp2(byte - 127.0)
    codes = (blocks / scale).astype(np.float32).astype(dtype).astype(np.float64)
    return np.moveaxis((codes * scale).reshape(v.shape), -1, axis)


WIDE = False


def mx_kscale(k):
    if not WIDE:
        return np.ones(k)
    levels = np.array([18, -18])
    if k % 512:
        return np.exp2(np.random.permutation(np.resize(levels, k // 32))).repeat(32)
    a = np.empty((k // 512, 16))
    for p in range(k // 512):
        a[p, :8] = np.random.permutation(np.resize(levels, 8))
        for g in range(8):
            far = levels[np.abs(levels - a[p, g]) >= 10]
            a[p, g + 8] = far[np.random.randint(len(far))]
    return np.exp2(a.ravel()).repeat(32)


BF16 = ml_dtypes.bfloat16


def bf(x):
    return np.asarray(x, np.float32).astype(BF16)


def f64(x):
    return np.asarray(x).astype(np.float64)


B, D0, D1, D2 = 512, 1024, 2048, 1024
DENSITY = 0.02


def setup_inputs():
    s = mx_kscale(B)[:, None]
    u = mx_kscale(D2)
    v = mx_kscale(D1)
    bound0 = np.sqrt(3.0 / (DENSITY * D0))
    bound1 = np.sqrt(6.0 / (DENSITY * D1))
    x0 = bf(np.random.standard_normal((B, D0)))
    W0_0 = bf(np.random.uniform(-bound0, bound0, (D1, D0)))
    b0 = bf(np.random.standard_normal(D1) * 0.3)
    m0 = bf(np.random.uniform(size=(D1, D0)) < DENSITY)
    W1_0 = bf(np.random.uniform(-bound1, bound1, (D2, D1)))
    b1 = bf(np.random.standard_normal(D2) * 0.3)
    m1 = bf(np.random.uniform(size=(D2, D1)) < DENSITY)
    g = bf(4.0 * np.random.standard_normal((B, D2)) * np.exp2(np.random.randint(-6, 1, (B, 1))) / s * u)
    pre0 = f64(x0) @ (f64(W0_0) * f64(m0)).T + f64(b0)
    pre1 = np.maximum(pre0, 0.0) @ (f64(W1_0) * f64(m1)).T + f64(b1)
    return {"x": bf(f64(x0) * s),
            "W0": bf(f64(W0_0) / v[:, None]),
            "b0": b0,
            "m0": m0,
            "W1": bf(f64(W1_0) * v[None, :] / u[:, None]),
            "b1": b1,
            "m1": m1,
            "pre0": np.asarray(pre0, np.float32),
            "pre1": np.asarray(pre1, np.float32),
            "grad_out": g}


def reference(x, W0, b0, m0, W1, b1, m1, pre0, pre1, grad_out):
    w0 = f64(W0) * f64(m0)
    w1 = f64(W1) * f64(m1)
    dz2 = f64(grad_out) * (f64(pre1) > 0.0)
    dh = mxq(dz2, 1, "e5m2") @ mxq(w1, 0, "e4m3")
    dz1 = dh * (f64(pre0) > 0.0)
    dx = mxq(dz1, 1, "e5m2") @ mxq(w0, 0, "e4m3")
    dW0 = (mxq(dz1, 0, "e5m2").T @ mxq(f64(x), 0, "e4m3")) * f64(m0)
    return dx, dW0

@@ -1,0 +1,291 @@
+from contextlib import ExitStack
+
+import concourse.mybir as mybir
+from concourse.masks import make_identity
+
+B, D0, D1, D2 = 512, 1024, 2048, 1024
+
+FLOPS = 3 * 2 * B * D1 * max(D0, D2)
+BYTES = 2 * (B * D0 + 2 * D1 * D0 + 2 * D2 * D1 + B * D2) + 4 * (B * D1 + B * D2) + 4 * (B * D0 + D1 * D0)
+
+F32 = mybir.dt.float32
+BF16 = mybir.dt.bfloat16
+U32 = mybir.dt.uint32
+U8 = mybir.dt.uint8
+E4M3X4 = mybir.dt.float8_e4m3fn_x4
+E5M2X4 = mybir.dt.float8_e5m2_x4
+GT = mybir.AluOpType.is_gt
+MULT = mybir.AluOpType.mult
+
+P = 128
+T = 4
+K_PASS = P * T
+NQ = D1 // K_PASS
+NG = D2 // K_PASS
+HALF = 512
+NBIG = 8
+NOUT = 8
+
+
+def tile_patchedsparsenetwork_pa_v_kernel(tc, x, W0, b0, m0, W1, b1, m1, pre0, pre1, grad_out, out_0, out_1):
+    nc = tc.nc
+    with ExitStack() as ctx:
+        keep = ctx.enter_context(tc.tile_pool(name="keep", bufs=1))
+        ring = ctx.enter_context(tc.tile_pool(name="ring", bufs=1))
+        work = ctx.enter_context(tc.tile_pool(name="work", bufs=2))
+        psum = ctx.enter_context(tc.psum_pool(name="psum", bufs=4))
+
+        ident_b = keep.tile([P, P], BF16, name="ident_b")
+        ident_f = keep.tile([P, P], F32, name="ident_f")
+        make_identity(nc, ident_f[:])
+        make_identity(nc, ident_b[:])
+
+        dz2_codes = keep.tile([P, NG, B], U32, name="dz2_codes", align_bytes=64)
+        dz2_scales = keep.tile([P, NG, B], U8, name="dz2_scales", align_bytes=64)
+        dz1f_codes = keep.tile([P, NQ, B], U32, name="dz1f_codes", align_bytes=64)
+        dz1f_scales = keep.tile([P, NQ, B], U8, name="dz1f_scales", align_bytes=64)
+        dz1t_codes = keep.tile([P, D1], U32, name="dz1t_codes", align_bytes=64)
+        dz1t_scales = keep.tile([P, D1], U8, name="dz1t_scales", align_bytes=64)
+        x_codes = keep.tile([P, D0], U32, name="x_codes", align_bytes=64)
+        x_scales = keep.tile([P, D0], U8, name="x_scales", align_bytes=64)
+        w0_codes = keep.tile([P, NQ, D0], U32, name="w0_codes", align_bytes=64)
+        w0_scales = keep.tile([P, NQ, D0], U8, name="w0_scales", align_bytes=64)
+
+        pre1_v = pre1.rearrange("(p j) w -> p j w", j=T)
+        grad_v = grad_out.rearrange("(p j) w -> p j w", j=T)
+        pre0_v = pre0.rearrange("(p j) w -> p j w", j=T)
+        x_v = x.rearrange("(p j) w -> p j w", j=T)
+        w1_v = W1.rearrange("(g p j) w -> g p j w", p=P, j=T)
+        m1_v = m1.rearrange("(g p j) w -> g p j w", p=P, j=T)
+        w0_v = W0.rearrange("(g p j) w -> g p j w", p=P, j=T)
+        m0_v = m0.rearrange("(g p j) w -> g p j w", p=P, j=T)
+        out0_v = out_0.rearrange("(p j) w -> p j w", j=T)
+        out1_v = out_1.rearrange("(g p j) w -> g p j w", p=P, j=T)
+
+        grad_in = ring.tile([P, T, D2], BF16, name="grad_in", tag="big", bufs=NBIG, align_bytes=64)
+        def load_dz(j):
+            a = work.tile([P, D2], F32, name=f"pre1_{j}", tag="outs", bufs=NOUT)
+            nc.sync.dma_start(out=a[:], in_=pre1_v[:, j, :])
+            nc.sync.dma_start(out=grad_in[:, j, :], in_=grad_v[:, j, :])
+            return a, grad_in[:, j, :]
+
+        def load_w1(k):
+            q, g = k // NG, k % NG
+            a = ring.tile([P, T, HALF], BF16, name=f"w1_{k}", tag="w1", bufs=3)
+            b = ring.tile([P, T, HALF], BF16, name=f"m1_{k}", tag="m1", bufs=3)
+            cols = slice(q * HALF, (q + 1) * HALF)
+            nc.sync.dma_start(out=a[:], in_=w1_v[g, :, :, cols])
+            nc.sync.dma_start(out=b[:], in_=m1_v[g, :, :, cols])
+            return a, b
+
+        def load_pre0(q):
+            a = ring.tile([P, T, HALF], F32, name=f"pre0_{q}", tag="big", bufs=NBIG, align_bytes=64)
+            nc.sync.dma_start(out=a[:], in_=pre0_v[:, :, q * HALF:(q + 1) * HALF])
+            return a
+
+        def load_big(src, nm):
+            a = ring.tile([P, T, D0], BF16, name=nm, tag="big", bufs=NBIG, align_bytes=64)
+            nc.sync.dma_start(out=a[:], in_=src)
+            return a
+
+        dz2_grouped = ring.tile([P, NG, T, P, T], BF16, name="dz2_grouped", tag="big", bufs=NBIG, align_bytes=64)
+
+        def make_dz2(j, pre, grad):
+            dz = work.tile([P, D2], BF16, name=f"dz2_{j}", tag="dz2", bufs=2)
+            nc.vector.scalar_tensor_tensor(out=dz[:], in0=pre[:], scalar=0.0, in1=grad, op0=GT, op1=MULT)
+            bank = psum.tile([P, NG, 2, P], F32, name=f"dz2T_{j}", tag="tp", bufs=3)
+            words = dz[:].bitcast(F32)
+            for g in range(NG):
+                for u in range(2):
+                    nc.tensor.transpose(bank[:, g, u, :], words[:, 256 * g + u:256 * (g + 1):2], ident_f[:])
+            nc.scalar.copy(
+                out=dz2_grouped[:, :, j].bitcast(F32),
+                in_=bank[:].rearrange("p g u m -> p g m u"))
+
+        def quant_dz2(g):
+            nc.vector.quantize_mx(out=dz2_codes[:, g, :].bitcast(E5M2X4), scales=dz2_scales[:, g, :],
+                                  in_=dz2_grouped[:, g].rearrange("p j m t -> p (j m t)"))
+
+        def mask_mult(a, b, cols):
+            prod = work.tile([P, T, HALF], BF16, name="prod", tag="prod", bufs=3)
+            nc.vector.tensor_tensor(out=prod[:], in0=a[:, :, cols], in1=b[:, :, cols], op=MULT)
+            return prod
+
+        def interleave_pe(prod):
+            grouped = work.tile([P, HALF, T], BF16, name="grouped", tag="grouped", bufs=3, align_bytes=64)
+            for c in range(2):
+                bank = psum.tile([P, 256, T], BF16, name="ibank", tag="tp", bufs=3)
+                for h in range(2):
+                    cols = slice(256 * c + 128 * h, 256 * c + 128 * (h + 1))
+                    nc.tensor.matmul(out=bank[:, 128 * h:128 * (h + 1), :], lhsT=ident_b[:],
+                                     rhs=prod[:, :, cols].rearrange("p j w -> p w j"), start=True, stop=True)
+                nc.scalar.copy(out=grouped[:, 256 * c:256 * (c + 1), :], in_=bank[:])
+            return grouped
+
+        def interleave_act(src):
+            grouped = work.tile([P, HALF, T], BF16, name="grouped", tag="grouped", bufs=3, align_bytes=64)
+            nc.scalar.copy(out=grouped[:], in_=src.rearrange("p j w -> p w j"))
+            return grouped
+
+        def quant(codes, scales, grouped, fmt):
+            nc.vector.quantize_mx(out=codes.bitcast(fmt), scales=scales, in_=grouped[:].rearrange("p w j -> p (w j)"))
+
+        def quant_w1(grouped):
+            codes = work.tile([P, HALF], U32, name="w1c", tag="w1c", bufs=4, align_bytes=64)
+            scales = work.tile([P, HALF], U8, name="w1s", tag="w1s", bufs=4, align_bytes=64)
+            quant(codes[:], scales[:], grouped, E4M3X4)
+            return codes, scales
+
+        def mm_dh(w1q):
+            banks = []
+            for j in range(T):
+                bank = psum.tile([P, HALF], F32, name="dh", tag="mm", bufs=3)
+                cols = slice(j * P, (j + 1) * P)
+                for g in (1, 0):
+                    codes, scales = w1q[g]
+                    nc.tensor.matmul_mx(out=bank[:], lhsT=dz2_codes[:, g, cols].bitcast(E5M2X4), lhsT_scale=dz2_scales[:, g, cols],
+                                        rhs=codes[:].bitcast(E4M3X4), rhs_scale=scales[:], start=(g == 1), stop=(g == 0))
+                banks.append(bank)
+            return banks
+
+        def mask_dz1(banks, pre):
+            dz1 = work.tile([P, T, HALF], BF16, name="dz1", tag="dz1", bufs=2)
+            for j in range(T):
+                nc.vector.scalar_tensor_tensor(out=dz1[:, j, :], in0=pre[:, j, :], scalar=0.0, in1=banks[j][:], op0=GT, op1=MULT)
+            return dz1
+
+        def tok_group(dz1):
+            grouped = work.tile([P, T, P, T], BF16, name="tokg", tag="tokg", bufs=1, align_bytes=64)
+            nc.scalar.copy(out=grouped[:], in_=dz1[:].rearrange("p t (m c) -> p c m t", c=T))
+            return grouped
+
+        def feat_group(dz1):
+            grouped = work.tile([P, T, P, T], BF16, name="featg", tag="featg", bufs=1, align_bytes=64)
+            for jp in range(2):
+                bank = psum.tile([P, 2, 2, P], F32, name="fbank", tag="tp", bufs=3)
+                for jl in range(2):
+                    words = dz1[:, 2 * jp + jl, :].bitcast(F32)
+                    for u in range(2):
+                        nc.tensor.transpose(bank[:, jl, u, :], words[:, u:256:2], ident_f[:])
+                nc.scalar.copy(out=grouped[:, 2 * jp:2 * jp + 2].bitcast(F32), in_=bank[:].rearrange("p j u m -> p j m u"))
+            return grouped
+
+        def quant_dz1(q, tokg, featg):
+            cols = slice(q * HALF, (q + 1) * HALF)
+            nc.vector.quantize_mx(out=dz1f_codes[:, q, :].bitcast(E5M2X4), scales=dz1f_scales[:, q, :],
+                                  in_=featg[:].rearrange("p j m t -> p (j m t)"))
+            nc.vector.quantize_mx(out=dz1t_codes[:, cols].bitcast(E5M2X4), scales=dz1t_scales[:, cols],
+                                  in_=tokg[:].rearrange("p c m t -> p (c m t)"))
+
+        def dw_tile(q, c, mask):
+            st = work.tile([P, D0], F32, name="dw", tag="outs", bufs=NOUT)
+            for n in range(2):
+                cols = slice(n * HALF, (n + 1) * HALF)
+                rows = slice(q * HALF + c * P, q * HALF + (c + 1) * P)
+                bank = psum.tile([P, HALF], F32, name="dwb", tag="mm", bufs=3)
+                nc.tensor.matmul_mx(out=bank[:], lhsT=dz1t_codes[:, rows].bitcast(E5M2X4), lhsT_scale=dz1t_scales[:, rows],
+                                    rhs=x_codes[:, cols].bitcast(E4M3X4), rhs_scale=x_scales[:, cols], start=True, stop=True)
+                nc.vector.tensor_tensor(out=st[:, cols], in0=bank[:], in1=mask[:, c, cols], op=MULT)
+            nc.sync.dma_start(out=out1_v[q, :, c, :], in_=st[:])
+
+        def dx_tile(j):
+            st = work.tile([P, D0], F32, name="dx", tag="outs", bufs=NOUT)
+            for n in range(2):
+                cols = slice(n * HALF, (n + 1) * HALF)
+                rows = slice(j * P, (j + 1) * P)
+                bank = psum.tile([P, HALF], F32, name="dxb", tag="dx", bufs=2)
+                for q in range(NQ):
+                    nc.tensor.matmul_mx(out=bank[:], lhsT=dz1f_codes[:, q, rows].bitcast(E5M2X4), lhsT_scale=dz1f_scales[:, q, rows],
+                                        rhs=w0_codes[:, q, cols].bitcast(E4M3X4), rhs_scale=w0_scales[:, q, cols],
+                                        start=(q == 0), stop=(q == NQ - 1))
+                nc.scalar.copy(out=st[:, cols], in_=bank[:])
+            nc.sync.dma_start(out=out0_v[:, j, :], in_=st[:])
+
+
+        dzin, w1in, pre0in, m0in, w0in, xin = {}, {}, {}, {}, {}, {}
+        order = [
+            ("dz", 0), ("dz", 1), ("dz", 2), ("dz", 3), ("w1", 0), ("w1", 1), ("pre0", 0), ("x", 0), ("m0", 0), ("w0", 0), ("w1", 2), ("w1", 3),
+            ("pre0", 1), ("m0", 1), ("w0", 1), ("w1", 4), ("w1", 5), ("m0", 2), ("w0", 2), ("pre0", 2), ("w1", 6), ("m0", 3), ("w0", 3), ("w1", 7), ("pre0", 3)]
+
+        def pump(n):
+            for i_load in range(n):
+                if order:
+                    kind, i = order.pop(0)
+                    if kind == "dz":
+                        dzin[i] = load_dz(i)
+                    elif kind == "w1":
+                        w1in[i] = load_w1(i)
+                    elif kind == "pre0":
+                        pre0in[i] = load_pre0(i)
+                    elif kind == "x":
+                        xin[i] = load_big(x_v, "x_in")
+                    elif kind == "m0":
+                        m0in[i] = load_big(m0_v[i], f"m0_{i}")
+                    else:
+                        w0in[i] = load_big(w0_v[i], f"w0_{i}")
+
+        full = slice(0, HALF)
+        grouped, w1q, w0g, xg = {}, {}, {}, {}
+
+        def w1_prep(k):
+            if k < 2 * NQ:
+                grouped[k] = interleave_pe(mask_mult(*w1in[k], full))
+
+        def w1_quant(k):
+            w1q[k] = quant_w1(grouped[k])
+
+        def half(n):
+            return slice(n * HALF, (n + 1) * HALF)
+
+        def w0_prep(q, n):
+            w0g[q, n] = interleave_act(mask_mult(w0in[q], m0in[q], half(n))[:])
+
+        def w0_quant(q, n):
+            quant(w0_codes[:, q, half(n)], w0_scales[:, q, half(n)], w0g[q, n], E4M3X4)
+
+        def x_prep(n):
+            xg[n] = interleave_act(xin[0][:, :, half(n)])
+
+        def x_quant(n):
+            quant(x_codes[:, half(n)], x_scales[:, half(n)], xg[n], E4M3X4)
+
+        def dw(q, c):
+            if q >= 0:
+                dw_tile(q, c, m0in[q])
+
+        pump(3)
+        make_dz2(0, *dzin[0])
+        pump(1)
+        for j in range(1, T):
+            make_dz2(j, *dzin[j])
+        pump(99)
+        quant_dz2(0)
+        quant_dz2(1)
+
+        plan = [[],[0,1],[2,3],[4],[5,6,7,8,9,10,11,12,13,14,15]]
+        for q in range(NQ):
+            w1_prep(2 * q)
+            w1_prep(2 * q + 1)
+            w1_quant(2 * q)
+            w1_quant(2 * q + 1)
+            banks = mm_dh([w1q[2 * q], w1q[2 * q + 1]])
+            dz1 = mask_dz1(banks, pre0in[q])
+            tg = tok_group(dz1)
+            fg = feat_group(dz1)
+            if q == 0:
+                x_prep(0)
+                x_prep(1)
+            w0_prep(q, 0)
+            w0_prep(q, 1)
+            quant_dz1(q, tg, fg)
+            if q == 0:
+                x_quant(0)
+                x_quant(1)
+            w0_quant(q, 0)
+            w0_quant(q, 1)
+            for d in plan[q]:
+                dw(d // 4, d % 4)
+        for d in plan[4]:
+            dw(d // 4, d % 4)
+        for j in range(T):
+            dx_tile(j)

@@ -26,30 +26,46 @@ HALF = 512
 NBIG = 8
 NOUT = 8
 
+ORDER = """
+lg.2 lw.0 lm.1 lp.2 lm.0 lg.1 lp.1 lw.1 lp.0 lg.0 lx lm.2 lw.2 m1.0 lp.3 dzV.2 i1.0 lg.3 dzT.2 lm.3 m1.1 dzV.1
+lw.3 i1.1 l0.0 dzV.0 dzT.1 dzS.1 lW.0 xi.0 dzS.2 dzT.0 lM.0 xq.0 xi.1 lm.4 m1.2 q1.0 lw.4 l0.1 dzV.3 dzS.0 xq.1
+lw.5 dzT.3 q1.1 dzS.3 lm.5 i1.2 qd.0 qd.1 m1.3 dh.0.2 lw.7 dh.0.3 mk.0.2 i1.3 dh.0.1 dh.0.0 mk.0.1 mk.0.3 lM.1
+mk.0.0 ft.0.1 q1.2 tk.0 q1.3 lm.7 m0.0 lW.1 i0.0 qt.0 dp.0.1 lm.6 m1.4 ft.0.0 dp.1.1 dv.0.1 dh.1.3 i1.4 m0.1
+dp.3.0 dp.3.1 lw.6 dh.1.1 dv.3.1 mk.1.3 l0.2 dp.0.0 q0.0 i0.1 lM.2 m1.5 mk.1.1 lW.2 dv.3.0 fs.0.0 dv.0.0 dp.2.1
+dh.1.2 i1.5 q1.4 dh.1.0 lM.3 mk.1.2 mk.1.0 m1.7 lW.3 tk.1 q0.1 dv.1.1 q1.5 m0.2 dh.2.3 i1.7 qt.1 m1.6 dp.4.0
+dh.2.2 dp.4.1 dv.2.1 i1.6 m0.3 dp.5.1 dh.2.1 mk.2.2 dv.4.0 mk.2.3 dp.6.1 fs.0.1 ft.1.1 dv.4.1 i0.2 ft.1.0
+dv.6.1 ds.4 l0.3 ds.0 ds.3 mk.2.1 dh.2.0 qf.0 dp.2.0 q1.6 fs.1.1 q0.2 i0.3 m0.4 mk.2.0 dv.5.1 fs.1.0 q1.7 tk.2
+dv.2.0 dh.3.0 m0.5 ft.2.0 ft.2.1 qf.1 dh.3.2 m0.7 dh.3.1 fs.2.1 dp.7.0 fs.2.0 qt.2 i0.7 mk.3.0 dp.11.1 dp.8.1
+dv.7.0 mk.3.1 dp.5.0 dh.3.3 qf.2 ft.3.0 dv.11.1 i0.5 mk.3.2 dp.10.1 xp.0.0 dv.8.1 mk.3.3 dp.8.0 xp.2.0 dv.10.1
+xp.4.0 tk.3 q0.7 dp.6.0 xp.0.1 dv.8.0 ft.3.1 dv.6.0 ds.8 dp.1.0 dv.5.0 dp.11.0 q0.3 ds.5 dp.9.0 ds.2 fs.3.1
+dv.11.0 fs.3.0 xp.1.0 dv.1.0 ds.11 dp.10.0 i0.4 xp.3.0 dv.10.0 ds.1 ds.6 qt.3 ds.10 m0.6 dp.13.0 dp.9.1 xp.3.1
+q0.5 i0.6 q0.4 xp.3.2 xp.4.1 dv.9.0 xp.1.1 xp.2.1 qf.3 xp.1.2 dp.13.1 dv.9.1 xp.0.2 dv.13.0 ds.9 dp.14.1 xp.1.3
+dv.13.1 dp.12.0 xs.1 xp.3.3 q0.6 ds.13 dv.14.1 xp.0.3 dp.12.1 xs.0 xp.4.2 dv.12.1 xp.5.0 xs.3 do.0 dp.14.0
+dv.12.0 xp.6.0 xp.2.2 dv.14.0 ds.12 dp.7.1 xp.2.3 dv.7.1 ds.14 xp.6.1 xs.2 ds.7 xp.6.2 do.1 xp.7.0 dp.15.1
+xp.5.1 xp.7.1 xp.4.3 dp.15.0 xs.4 xp.6.3 dv.15.0 xp.7.2 xp.5.2 dv.15.1 xp.7.3 xp.5.3 xs.7 ds.15 xs.5 xs.6 do.2
+do.3
+"""
+
 
 def tile_patchedsparsenetwork_pa_v_kernel(tc, x, W0, b0, m0, W1, b1, m1, pre0, pre1, grad_out, out_0, out_1):
     nc = tc.nc
     with ExitStack() as ctx:
         keep = ctx.enter_context(tc.tile_pool(name="keep", bufs=1))
-        ring = ctx.enter_context(tc.tile_pool(name="ring", bufs=1))
         work = ctx.enter_context(tc.tile_pool(name="work", bufs=2))
-        psum = ctx.enter_context(tc.psum_pool(name="psum", bufs=4))
+        psum = ctx.enter_context(tc.psum_pool(name="psum", bufs=1))
+        ctx.enter_context(tc.manual_schedule())
 
-        ident_b = keep.tile([P, P], BF16, name="ident_b")
         ident_f = keep.tile([P, P], F32, name="ident_f")
         make_identity(nc, ident_f[:])
-        make_identity(nc, ident_b[:])
 
-        dz2_codes = keep.tile([P, NG, B], U32, name="dz2_codes", align_bytes=64)
-        dz2_scales = keep.tile([P, NG, B], U8, name="dz2_scales", align_bytes=64)
-        dz1f_codes = keep.tile([P, NQ, B], U32, name="dz1f_codes", align_bytes=64)
-        dz1f_scales = keep.tile([P, NQ, B], U8, name="dz1f_scales", align_bytes=64)
-        dz1t_codes = keep.tile([P, D1], U32, name="dz1t_codes", align_bytes=64)
-        dz1t_scales = keep.tile([P, D1], U8, name="dz1t_scales", align_bytes=64)
-        x_codes = keep.tile([P, D0], U32, name="x_codes", align_bytes=64)
-        x_scales = keep.tile([P, D0], U8, name="x_scales", align_bytes=64)
-        w0_codes = keep.tile([P, NQ, D0], U32, name="w0_codes", align_bytes=64)
-        w0_scales = keep.tile([P, NQ, D0], U8, name="w0_scales", align_bytes=64)
+        def plane(width, nm, dtype):
+            return keep.tile([P, width], dtype, name=nm, align_bytes=64)
+
+        dz2_codes, dz2_scales = plane(NG * B, "dz2_codes", U32), plane(NG * B, "dz2_scales", U8)
+        dz1f_codes, dz1f_scales = plane(NQ * B, "dz1f_codes", U32), plane(NQ * B, "dz1f_scales", U8)
+        dz1t_codes, dz1t_scales = plane(D1, "dz1t_codes", U32), plane(D1, "dz1t_scales", U8)
+        x_codes, x_scales = plane(D0, "x_codes", U32), plane(D0, "x_scales", U8)
+        w0_codes, w0_scales = plane(NQ * D0, "w0_codes", U32), plane(NQ * D0, "w0_scales", U8)
 
         pre1_v = pre1.rearrange("(p j) w -> p j w", j=T)
         grad_v = grad_out.rearrange("(p j) w -> p j w", j=T)
@@ -62,230 +78,191 @@ def tile_patchedsparsenetwork_pa_v_kernel(tc, x, W0, b0, m0, W1, b1, m1, pre0, p
         out0_v = out_0.rearrange("(p j) w -> p j w", j=T)
         out1_v = out_1.rearrange("(g p j) w -> g p j w", p=P, j=T)
 
-        grad_in = ring.tile([P, T, D2], BF16, name="grad_in", tag="big", bufs=NBIG, align_bytes=64)
-        def load_dz(j):
-            a = work.tile([P, D2], F32, name=f"pre1_{j}", tag="outs", bufs=NOUT)
-            nc.sync.dma_start(out=a[:], in_=pre1_v[:, j, :])
-            nc.sync.dma_start(out=grad_in[:, j, :], in_=grad_v[:, j, :])
-            return a, grad_in[:, j, :]
+        live = {}
 
-        def load_w1(k):
-            q, g = k // NG, k % NG
-            a = ring.tile([P, T, HALF], BF16, name=f"w1_{k}", tag="w1", bufs=3)
-            b = ring.tile([P, T, HALF], BF16, name=f"m1_{k}", tag="m1", bufs=3)
-            cols = slice(q * HALF, (q + 1) * HALF)
-            nc.sync.dma_start(out=a[:], in_=w1_v[g, :, :, cols])
-            nc.sync.dma_start(out=b[:], in_=m1_v[g, :, :, cols])
-            return a, b
+        def part(i, width):
+            return slice(i * width, (i + 1) * width)
 
-        def load_pre0(q):
-            a = ring.tile([P, T, HALF], F32, name=f"pre0_{q}", tag="big", bufs=NBIG, align_bytes=64)
-            nc.sync.dma_start(out=a[:], in_=pre0_v[:, :, q * HALF:(q + 1) * HALF])
-            return a
+        def get(key, make):
+            if key not in live:
+                live[key] = make()
+            return live[key]
 
-        def load_big(src, nm):
-            a = ring.tile([P, T, D0], BF16, name=nm, tag="big", bufs=NBIG, align_bytes=64)
-            nc.sync.dma_start(out=a[:], in_=src)
-            return a
+        def sb(tag, shape, dtype, bufs):
+            return work.tile(shape, dtype, name=tag, tag=tag, bufs=bufs, align_bytes=64)
 
-        dz2_grouped = ring.tile([P, NG, T, P, T], BF16, name="dz2_grouped", tag="big", bufs=NBIG, align_bytes=64)
+        def ps(tag, shape, dtype, bufs):
+            return psum.tile(shape, dtype, name=tag, tag=tag, bufs=bufs)
 
-        def make_dz2(j, pre, grad):
-            dz = work.tile([P, D2], BF16, name=f"dz2_{j}", tag="dz2", bufs=2)
-            nc.vector.scalar_tensor_tensor(out=dz[:], in0=pre[:], scalar=0.0, in1=grad, op0=GT, op1=MULT)
-            bank = psum.tile([P, NG, 2, P], F32, name=f"dz2T_{j}", tag="tp", bufs=3)
-            words = dz[:].bitcast(F32)
+        def big():
+            return sb("big", [P, 4 * 1024], BF16, NBIG)
+
+        def lp(j):
+            live["pre1", j] = sb("outs", [P, D2], F32, NOUT)
+            nc.sync.dma_start(out=live["pre1", j][:], in_=pre1_v[:, j, :])
+
+        def lg(j):
+            grad = get("grad", big)
+            nc.sync.dma_start(out=grad[:, part(j, D2)], in_=grad_v[:, j, :])
+
+        def lw(k):
+            t = get(("w1", k), lambda: sb("w1", [P, 2, T, HALF], BF16, 4))
+            nc.sync.dma_start(out=t[:, 0], in_=w1_v[k % NG, :, :, part(k // NG, HALF)])
+
+        def lm(k):
+            t = get(("w1", k), lambda: sb("w1", [P, 2, T, HALF], BF16, 4))
+            nc.sync.dma_start(out=t[:, 1], in_=m1_v[k % NG, :, :, part(k // NG, HALF)])
+
+        def l0(c):
+            live["pre0", c] = sb("big", [P, T, HALF], F32, NBIG)
+            nc.sync.dma_start(out=live["pre0", c][:], in_=pre0_v[:, :, part(c, HALF)])
+
+        def lM(c):
+            live["m0", c] = sb("big", [P, T, D0], BF16, NBIG)
+            nc.sync.dma_start(out=live["m0", c][:], in_=m0_v[c])
+
+        def lW(c):
+            live["w0", c] = sb("big", [P, T, D0], BF16, NBIG)
+            nc.sync.dma_start(out=live["w0", c][:], in_=w0_v[c])
+
+        def lx():
+            live["x"] = sb("big", [P, T, D0], BF16, NBIG)
+            nc.sync.dma_start(out=live["x"][:], in_=x_v)
+
+        def dzV(j):
+            live["dz2", j] = sb("dz2", [P, D2], BF16, 2)
+            nc.vector.scalar_tensor_tensor(out=live["dz2", j][:], in0=live["pre1", j][:], scalar=0.0,
+                                           in1=live["grad"][:, part(j, D2)], op0=GT, op1=MULT)
+
+        def dzT(j):
+            bank = ps("tp", [P, NG, 2, P], F32, 2)
+            live["dzb", j] = bank
+            words = live["dz2", j][:].bitcast(F32)
             for g in range(NG):
                 for u in range(2):
                     nc.tensor.transpose(bank[:, g, u, :], words[:, 256 * g + u:256 * (g + 1):2], ident_f[:])
-            nc.scalar.copy(
-                out=dz2_grouped[:, :, j].bitcast(F32),
-                in_=bank[:].rearrange("p g u m -> p g m u"))
 
-        def quant_dz2(g):
-            nc.vector.quantize_mx(out=dz2_codes[:, g, :].bitcast(E5M2X4), scales=dz2_scales[:, g, :],
-                                  in_=dz2_grouped[:, g].rearrange("p j m t -> p (j m t)"))
+        def dzS(j):
+            grouped = get("dz2g", lambda: sb("big", [P, NG, T, P, T], BF16, NBIG))
+            nc.scalar.copy(out=grouped[:, :, j].bitcast(F32), in_=live["dzb", j][:].rearrange("p g u m -> p g m u"))
 
-        def mask_mult(a, b, cols):
-            prod = work.tile([P, T, HALF], BF16, name="prod", tag="prod", bufs=3)
-            nc.vector.tensor_tensor(out=prod[:], in0=a[:, :, cols], in1=b[:, :, cols], op=MULT)
+        def qd(g):
+            nc.vector.quantize_mx(out=dz2_codes[:, part(g, B)].bitcast(E5M2X4), scales=dz2_scales[:, part(g, B)],
+                                  in_=live["dz2g"][:, g].rearrange("p j m t -> p (j m t)"))
+
+        def mask_mult(a, b):
+            prod = sb("prod", [P, T, HALF], BF16, 3)
+            nc.vector.tensor_tensor(out=prod[:], in0=a, in1=b, op=MULT)
             return prod
 
-        def interleave_pe(prod):
-            grouped = work.tile([P, HALF, T], BF16, name="grouped", tag="grouped", bufs=3, align_bytes=64)
-            for c in range(2):
-                bank = psum.tile([P, 256, T], BF16, name="ibank", tag="tp", bufs=3)
-                for h in range(2):
-                    cols = slice(256 * c + 128 * h, 256 * c + 128 * (h + 1))
-                    nc.tensor.matmul(out=bank[:, 128 * h:128 * (h + 1), :], lhsT=ident_b[:],
-                                     rhs=prod[:, :, cols].rearrange("p j w -> p w j"), start=True, stop=True)
-                nc.scalar.copy(out=grouped[:, 256 * c:256 * (c + 1), :], in_=bank[:])
+        def interleave(copy, src):
+            grouped = sb("grouped", [P, HALF, T], BF16, 3)
+            copy(out=grouped[:], in_=src.rearrange("p t w -> p w t"))
             return grouped
 
-        def interleave_act(src):
-            grouped = work.tile([P, HALF, T], BF16, name="grouped", tag="grouped", bufs=3, align_bytes=64)
-            nc.scalar.copy(out=grouped[:], in_=src.rearrange("p j w -> p w j"))
-            return grouped
+        def quant(codes, scales, grouped):
+            nc.vector.quantize_mx(out=codes.bitcast(E4M3X4), scales=scales, in_=grouped[:].rearrange("p w t -> p (w t)"))
 
-        def quant(codes, scales, grouped, fmt):
-            nc.vector.quantize_mx(out=codes.bitcast(fmt), scales=scales, in_=grouped[:].rearrange("p w j -> p (w j)"))
+        def mul1(k):
+            t = live["w1", k]
+            live["pr", k] = mask_mult(t[:, 0], t[:, 1])
 
-        def quant_w1(grouped):
-            codes = work.tile([P, HALF], U32, name="w1c", tag="w1c", bufs=4, align_bytes=64)
-            scales = work.tile([P, HALF], U8, name="w1s", tag="w1s", bufs=4, align_bytes=64)
-            quant(codes[:], scales[:], grouped, E4M3X4)
-            return codes, scales
+        def i1(k):
+            live["gr", k] = interleave(nc.scalar.copy, live["pr", k][:])
 
-        def mm_dh(w1q):
-            banks = []
-            for j in range(T):
-                bank = psum.tile([P, HALF], F32, name="dh", tag="mm", bufs=3)
-                cols = slice(j * P, (j + 1) * P)
-                for g in (1, 0):
-                    codes, scales = w1q[g]
-                    nc.tensor.matmul_mx(out=bank[:], lhsT=dz2_codes[:, g, cols].bitcast(E5M2X4), lhsT_scale=dz2_scales[:, g, cols],
-                                        rhs=codes[:].bitcast(E4M3X4), rhs_scale=scales[:], start=(g == 1), stop=(g == 0))
-                banks.append(bank)
-            return banks
+        def q1(k):
+            codes = sb("w1c", [P, HALF], U32, 4)
+            scales = sb("w1s", [P, HALF], U8, 4)
+            quant(codes[:], scales[:], live["gr", k])
+            live["w1c", k] = codes, scales
 
-        def mask_dz1(banks, pre):
-            dz1 = work.tile([P, T, HALF], BF16, name="dz1", tag="dz1", bufs=2)
-            for j in range(T):
-                nc.vector.scalar_tensor_tensor(out=dz1[:, j, :], in0=pre[:, j, :], scalar=0.0, in1=banks[j][:], op0=GT, op1=MULT)
-            return dz1
+        def dh(c, j):
+            bank = ps("dh", [P, HALF], F32, 3)
+            live["dhb", c, j] = bank
+            for g in range(NG):
+                codes, scales = live["w1c", NG * c + g]
+                cols = slice(g * B + j * P, g * B + (j + 1) * P)
+                nc.tensor.matmul_mx(out=bank[:], lhsT=dz2_codes[:, cols].bitcast(E5M2X4), lhsT_scale=dz2_scales[:, cols],
+                                    rhs=codes[:].bitcast(E4M3X4), rhs_scale=scales[:], start=(g == 0), stop=(g == NG - 1))
 
-        def tok_group(dz1):
-            grouped = work.tile([P, T, P, T], BF16, name="tokg", tag="tokg", bufs=1, align_bytes=64)
-            nc.scalar.copy(out=grouped[:], in_=dz1[:].rearrange("p t (m c) -> p c m t", c=T))
-            return grouped
+        def mk(c, j):
+            dz1 = get(("dz1", c), lambda: sb("dz1", [P, T, HALF], BF16, 2))
+            nc.vector.scalar_tensor_tensor(out=dz1[:, j], in0=live["pre0", c][:, j], scalar=0.0, in1=live["dhb", c, j][:], op0=GT, op1=MULT)
 
-        def feat_group(dz1):
-            grouped = work.tile([P, T, P, T], BF16, name="featg", tag="featg", bufs=1, align_bytes=64)
-            for jp in range(2):
-                bank = psum.tile([P, 2, 2, P], F32, name="fbank", tag="tp", bufs=3)
-                for jl in range(2):
-                    words = dz1[:, 2 * jp + jl, :].bitcast(F32)
-                    for u in range(2):
-                        nc.tensor.transpose(bank[:, jl, u, :], words[:, u:256:2], ident_f[:])
-                nc.scalar.copy(out=grouped[:, 2 * jp:2 * jp + 2].bitcast(F32), in_=bank[:].rearrange("p j u m -> p j m u"))
-            return grouped
+        def ft(c, h):
+            bank = ps("tp", [P, 2, 2, P], F32, 2)
+            live["fb", c, h] = bank
+            for jl in range(2):
+                words = live["dz1", c][:, 2 * h + jl].bitcast(F32)
+                for u in range(2):
+                    nc.tensor.transpose(bank[:, jl, u, :], words[:, u:256:2], ident_f[:])
 
-        def quant_dz1(q, tokg, featg):
-            cols = slice(q * HALF, (q + 1) * HALF)
-            nc.vector.quantize_mx(out=dz1f_codes[:, q, :].bitcast(E5M2X4), scales=dz1f_scales[:, q, :],
-                                  in_=featg[:].rearrange("p j m t -> p (j m t)"))
-            nc.vector.quantize_mx(out=dz1t_codes[:, cols].bitcast(E5M2X4), scales=dz1t_scales[:, cols],
-                                  in_=tokg[:].rearrange("p c m t -> p (c m t)"))
+        def fs(c, h):
+            grouped = get(("fg", c), lambda: sb("featg", [P, T, P, T], BF16, 1))
+            nc.scalar.copy(out=grouped[:, 2 * h:2 * h + 2].bitcast(F32), in_=live["fb", c, h][:].rearrange("p j u m -> p j m u"))
 
-        def dw_tile(q, c, mask):
-            st = work.tile([P, D0], F32, name="dw", tag="outs", bufs=NOUT)
-            for n in range(2):
-                cols = slice(n * HALF, (n + 1) * HALF)
-                rows = slice(q * HALF + c * P, q * HALF + (c + 1) * P)
-                bank = psum.tile([P, HALF], F32, name="dwb", tag="mm", bufs=3)
-                nc.tensor.matmul_mx(out=bank[:], lhsT=dz1t_codes[:, rows].bitcast(E5M2X4), lhsT_scale=dz1t_scales[:, rows],
-                                    rhs=x_codes[:, cols].bitcast(E4M3X4), rhs_scale=x_scales[:, cols], start=True, stop=True)
-                nc.vector.tensor_tensor(out=st[:, cols], in0=bank[:], in1=mask[:, c, cols], op=MULT)
-            nc.sync.dma_start(out=out1_v[q, :, c, :], in_=st[:])
+        def tk(c):
+            live["tg", c] = sb("tokg", [P, T, P, T], BF16, 1)
+            nc.scalar.copy(out=live["tg", c][:], in_=live["dz1", c][:].rearrange("p t (m c) -> p c m t", c=T))
 
-        def dx_tile(j):
-            st = work.tile([P, D0], F32, name="dx", tag="outs", bufs=NOUT)
-            for n in range(2):
-                cols = slice(n * HALF, (n + 1) * HALF)
-                rows = slice(j * P, (j + 1) * P)
-                bank = psum.tile([P, HALF], F32, name="dxb", tag="dx", bufs=2)
-                for q in range(NQ):
-                    nc.tensor.matmul_mx(out=bank[:], lhsT=dz1f_codes[:, q, rows].bitcast(E5M2X4), lhsT_scale=dz1f_scales[:, q, rows],
-                                        rhs=w0_codes[:, q, cols].bitcast(E4M3X4), rhs_scale=w0_scales[:, q, cols],
-                                        start=(q == 0), stop=(q == NQ - 1))
-                nc.scalar.copy(out=st[:, cols], in_=bank[:])
-            nc.sync.dma_start(out=out0_v[:, j, :], in_=st[:])
+        def qf(c):
+            nc.vector.quantize_mx(out=dz1f_codes[:, part(c, B)].bitcast(E5M2X4), scales=dz1f_scales[:, part(c, B)],
+                                  in_=live["fg", c][:].rearrange("p j m t -> p (j m t)"))
 
+        def qt(c):
+            nc.vector.quantize_mx(out=dz1t_codes[:, part(c, HALF)].bitcast(E5M2X4), scales=dz1t_scales[:, part(c, HALF)],
+                                  in_=live["tg", c][:].rearrange("p c m t -> p (c m t)"))
 
-        dzin, w1in, pre0in, m0in, w0in, xin = {}, {}, {}, {}, {}, {}
-        order = [
-            ("dz", 0), ("dz", 1), ("dz", 2), ("dz", 3), ("w1", 0), ("w1", 1), ("pre0", 0), ("x", 0), ("m0", 0), ("w0", 0), ("w1", 2), ("w1", 3),
-            ("pre0", 1), ("m0", 1), ("w0", 1), ("w1", 4), ("w1", 5), ("m0", 2), ("w0", 2), ("pre0", 2), ("w1", 6), ("m0", 3), ("w0", 3), ("w1", 7), ("pre0", 3)]
+        def xi(n):
+            live["xg", n] = interleave(nc.vector.tensor_copy if n < 1 else nc.scalar.copy, live["x"][:, :, part(n, HALF)])
 
-        def pump(n):
-            for i_load in range(n):
-                if order:
-                    kind, i = order.pop(0)
-                    if kind == "dz":
-                        dzin[i] = load_dz(i)
-                    elif kind == "w1":
-                        w1in[i] = load_w1(i)
-                    elif kind == "pre0":
-                        pre0in[i] = load_pre0(i)
-                    elif kind == "x":
-                        xin[i] = load_big(x_v, "x_in")
-                    elif kind == "m0":
-                        m0in[i] = load_big(m0_v[i], f"m0_{i}")
-                    else:
-                        w0in[i] = load_big(w0_v[i], f"w0_{i}")
+        def xq(n):
+            quant(x_codes[:, part(n, HALF)], x_scales[:, part(n, HALF)], live["xg", n])
 
-        full = slice(0, HALF)
-        grouped, w1q, w0g, xg = {}, {}, {}, {}
+        def mul0(i):
+            q, n = i // 2, i % 2
+            live["p0", i] = mask_mult(live["w0", q][:, :, part(n, HALF)], live["m0", q][:, :, part(n, HALF)])
 
-        def w1_prep(k):
-            if k < 2 * NQ:
-                grouped[k] = interleave_pe(mask_mult(*w1in[k], full))
+        def i0(i):
+            live["g0", i] = interleave(nc.scalar.copy, live["p0", i][:])
 
-        def w1_quant(k):
-            w1q[k] = quant_w1(grouped[k])
+        def q0(i):
+            quant(w0_codes[:, part(i, HALF)], w0_scales[:, part(i, HALF)], live["g0", i])
 
-        def half(n):
-            return slice(n * HALF, (n + 1) * HALF)
+        def dp(i, n):
+            bank = ps("dw", [P, HALF], F32, 3)
+            live["dwb", i, n] = bank
+            rows, cols = part(i, P), part(n, HALF)
+            nc.tensor.matmul_mx(out=bank[:], lhsT=dz1t_codes[:, rows].bitcast(E5M2X4), lhsT_scale=dz1t_scales[:, rows],
+                                rhs=x_codes[:, cols].bitcast(E4M3X4), rhs_scale=x_scales[:, cols], start=True, stop=True)
 
-        def w0_prep(q, n):
-            w0g[q, n] = interleave_act(mask_mult(w0in[q], m0in[q], half(n))[:])
+        def dv(i, n):
+            st = get(("st", i), lambda: sb("outs", [P, D0], F32, NOUT))
+            nc.vector.tensor_tensor(out=st[:, part(n, HALF)], in0=live["dwb", i, n][:], in1=live["m0", i // T][:, i % T, part(n, HALF)], op=MULT)
 
-        def w0_quant(q, n):
-            quant(w0_codes[:, q, half(n)], w0_scales[:, q, half(n)], w0g[q, n], E4M3X4)
+        def ds(i):
+            nc.sync.dma_start(out=out1_v[i // T, :, i % T, :], in_=live["st", i][:])
 
-        def x_prep(n):
-            xg[n] = interleave_act(xin[0][:, :, half(n)])
+        def xp(b, r):
+            j, n = b // 2, b % 2
+            if r == 0:
+                tag, bufs = ("tp", 2) if b in (1, 3, 5, 7) else ("dh", 3)
+                live["dxb", b] = ps(tag, [P, HALF], F32, bufs)
+            rows = slice(r * B + j * P, r * B + (j + 1) * P)
+            cols = slice(r * D0 + n * HALF, r * D0 + (n + 1) * HALF)
+            nc.tensor.matmul_mx(out=live["dxb", b][:], lhsT=dz1f_codes[:, rows].bitcast(E5M2X4), lhsT_scale=dz1f_scales[:, rows],
+                                rhs=w0_codes[:, cols].bitcast(E4M3X4), rhs_scale=w0_scales[:, cols], start=(r == 0), stop=(r == NQ - 1))
 
-        def x_quant(n):
-            quant(x_codes[:, half(n)], x_scales[:, half(n)], xg[n], E4M3X4)
+        def xs(b):
+            st = get(("dst", b // 2), lambda: sb("outs", [P, D0], F32, NOUT))
+            nc.scalar.copy(out=st[:, part(b % 2, HALF)], in_=live["dxb", b][:])
 
-        def dw(q, c):
-            if q >= 0:
-                dw_tile(q, c, m0in[q])
+        def do(j):
+            nc.sync.dma_start(out=out0_v[:, j, :], in_=live["dst", j][:])
 
-        pump(3)
-        make_dz2(0, *dzin[0])
-        pump(1)
-        for j in range(1, T):
-            make_dz2(j, *dzin[j])
-        pump(99)
-        quant_dz2(0)
-        quant_dz2(1)
-
-        plan = [[],[0,1],[2,3],[4],[5,6,7,8,9,10,11,12,13,14,15]]
-        for q in range(NQ):
-            w1_prep(2 * q)
-            w1_prep(2 * q + 1)
-            w1_quant(2 * q)
-            w1_quant(2 * q + 1)
-            banks = mm_dh([w1q[2 * q], w1q[2 * q + 1]])
-            dz1 = mask_dz1(banks, pre0in[q])
-            tg = tok_group(dz1)
-            fg = feat_group(dz1)
-            if q == 0:
-                x_prep(0)
-                x_prep(1)
-            w0_prep(q, 0)
-            w0_prep(q, 1)
-            quant_dz1(q, tg, fg)
-            if q == 0:
-                x_quant(0)
-                x_quant(1)
-            w0_quant(q, 0)
-            w0_quant(q, 1)
-            for d in plan[q]:
-                dw(d // 4, d % 4)
-        for d in plan[4]:
-            dw(d // 4, d % 4)
-        for j in range(T):
-            dx_tile(j)
+        pieces = {"lp": lp, "lg": lg, "lw": lw, "lm": lm, "l0": l0, "lM": lM, "lW": lW, "lx": lx, "dzV": dzV, "dzT": dzT, "dzS": dzS,
+                  "qd": qd, "m1": mul1, "i1": i1, "q1": q1, "dh": dh, "mk": mk, "ft": ft, "fs": fs, "tk": tk, "qf": qf, "qt": qt,
+                  "xi": xi, "xq": xq, "m0": mul0, "i0": i0, "q0": q0, "dp": dp, "dv": dv, "ds": ds, "xp": xp, "xs": xs, "do": do}
+        for word in ORDER.split():
+            parts = word.split(".")
+            pieces[parts[0]](*[int(a) for a in parts[1:]])

@@ -23,27 +23,27 @@ K_PASS = P * T
 NQ = D1 // K_PASS
 NG = D2 // K_PASS
 HALF = 512
-NBIG = 8
-NOUT = 8
+SPLIT = (1, 3)
+NBIG = 6
+NOUT = 4
 
 ORDER = """
-lg.2 lw.0 lm.1 lp.2 lm.0 lg.1 lp.1 lw.1 lp.0 lg.0 lx lm.2 lw.2 m1.0 lp.3 dzV.2 i1.0 lg.3 dzT.2 lm.3 m1.1 dzV.1
-lw.3 i1.1 l0.0 dzV.0 dzT.1 dzS.1 lW.0 xi.0 dzS.2 dzT.0 lM.0 xq.0 xi.1 lm.4 m1.2 q1.0 lw.4 l0.1 dzV.3 dzS.0 xq.1
-lw.5 dzT.3 q1.1 dzS.3 lm.5 i1.2 qd.0 qd.1 m1.3 dh.0.2 lw.7 dh.0.3 mk.0.2 i1.3 dh.0.1 dh.0.0 mk.0.1 mk.0.3 lM.1
-mk.0.0 ft.0.1 q1.2 tk.0 q1.3 lm.7 m0.0 lW.1 i0.0 qt.0 dp.0.1 lm.6 m1.4 ft.0.0 dp.1.1 dv.0.1 dh.1.3 i1.4 m0.1
-dp.3.0 dp.3.1 lw.6 dh.1.1 dv.3.1 mk.1.3 l0.2 dp.0.0 q0.0 i0.1 lM.2 m1.5 mk.1.1 lW.2 dv.3.0 fs.0.0 dv.0.0 dp.2.1
-dh.1.2 i1.5 q1.4 dh.1.0 lM.3 mk.1.2 mk.1.0 m1.7 lW.3 tk.1 q0.1 dv.1.1 q1.5 m0.2 dh.2.3 i1.7 qt.1 m1.6 dp.4.0
-dh.2.2 dp.4.1 dv.2.1 i1.6 m0.3 dp.5.1 dh.2.1 mk.2.2 dv.4.0 mk.2.3 dp.6.1 fs.0.1 ft.1.1 dv.4.1 i0.2 ft.1.0
-dv.6.1 ds.4 l0.3 ds.0 ds.3 mk.2.1 dh.2.0 qf.0 dp.2.0 q1.6 fs.1.1 q0.2 i0.3 m0.4 mk.2.0 dv.5.1 fs.1.0 q1.7 tk.2
-dv.2.0 dh.3.0 m0.5 ft.2.0 ft.2.1 qf.1 dh.3.2 m0.7 dh.3.1 fs.2.1 dp.7.0 fs.2.0 qt.2 i0.7 mk.3.0 dp.11.1 dp.8.1
-dv.7.0 mk.3.1 dp.5.0 dh.3.3 qf.2 ft.3.0 dv.11.1 i0.5 mk.3.2 dp.10.1 xp.0.0 dv.8.1 mk.3.3 dp.8.0 xp.2.0 dv.10.1
-xp.4.0 tk.3 q0.7 dp.6.0 xp.0.1 dv.8.0 ft.3.1 dv.6.0 ds.8 dp.1.0 dv.5.0 dp.11.0 q0.3 ds.5 dp.9.0 ds.2 fs.3.1
-dv.11.0 fs.3.0 xp.1.0 dv.1.0 ds.11 dp.10.0 i0.4 xp.3.0 dv.10.0 ds.1 ds.6 qt.3 ds.10 m0.6 dp.13.0 dp.9.1 xp.3.1
-q0.5 i0.6 q0.4 xp.3.2 xp.4.1 dv.9.0 xp.1.1 xp.2.1 qf.3 xp.1.2 dp.13.1 dv.9.1 xp.0.2 dv.13.0 ds.9 dp.14.1 xp.1.3
-dv.13.1 dp.12.0 xs.1 xp.3.3 q0.6 ds.13 dv.14.1 xp.0.3 dp.12.1 xs.0 xp.4.2 dv.12.1 xp.5.0 xs.3 do.0 dp.14.0
-dv.12.0 xp.6.0 xp.2.2 dv.14.0 ds.12 dp.7.1 xp.2.3 dv.7.1 ds.14 xp.6.1 xs.2 ds.7 xp.6.2 do.1 xp.7.0 dp.15.1
-xp.5.1 xp.7.1 xp.4.3 dp.15.0 xs.4 xp.6.3 dv.15.0 xp.7.2 xp.5.2 dv.15.1 xp.7.3 xp.5.3 xs.7 ds.15 xs.5 xs.6 do.2
-do.3
+lg.0 lw.0.1 lm.0.1 lg.1 lp.1 lm.0.0 lw.0.0 lp.3 lg.2 lp.2 m1.1 lp.0 lg.3 i1.1 lx dzV.1 lW.0 q1.1 dzT.1 dzS.1
+m1.0 l0.0 lM.0 i1.0 lw.1.0 q1.0 lm.1.0 dzV.2 lm.1.1 dzV.0 dzT.2 lw.1.1 dzS.2 dzV.3 dzT.0 dzS.0 dzT.3 xi.1 l0.1
+dzS.3 qd.1 xq.1 qd.0 xi.0 dh.0.1 lM.1 dh.0.0 dh.0.3 xq.0 l0.2 mk.0.0 mk.0.3 dh.0.2 mk.0.1 mk.0.2 ft.0.0 m0.0
+tk.0 lW.1 ft.0.1 m0.1 i0.0 qt.0 dp.0.0 dp.3.0 dv.0.0 dp.0.1 dv.3.0 dp.1.0 dv.1.0 dp.3.1 i0.1 q0.0 dp.1.1 m1.4
+m1.2 i1.4 l0.3 m1.6 dv.3.1 dv.1.1 dp.2.1 i1.2 q1.4 dp.2.0 q0.1 dv.2.0 dv.0.1 i1.6 q1.2 ds.1 m1.3 m1.5 i1.3 m1.7
+q1.6 dv.2.1 i1.5 q1.3 ds.3 lW.3 dh.1.1 dh.1.0 mk.1.1 dh.1.3 mk.1.0 i1.7 dh.1.2 q1.5 mk.1.2 dh.2.0 mk.1.3 dh.2.2
+mk.2.0 lW.2 dh.2.3 mk.2.2 dh.2.1 fs.0.1 m0.2 fs.0.0 ft.1.1 tk.1 ft.1.0 q1.7 m0.3 dh.3.1 qf.0 mk.2.1 i0.3 mk.3.1
+dh.3.2 qt.1 dh.3.0 mk.2.3 dp.6.1 dp.6.0 dv.6.1 lM.3 dp.5.0 xp.4.0 dv.6.0 fs.1.1 dp.4.0 q0.3 dp.7.0 fs.1.0
+ft.2.0 dv.7.0 i0.2 ft.2.1 qf.1 mk.3.0 dp.5.1 dv.5.1 dh.3.3 dv.5.0 dp.4.1 fs.2.0 lM.2 q0.2 dp.7.1 tk.2 ft.3.0
+dv.7.1 xp.4.1 mk.3.3 ds.7 dv.4.1 xp.0.0 xp.0.1 mk.3.2 dv.4.0 xp.2.0 fs.2.1 xp.2.1 m0.6 ds.5 ft.3.1 qf.2 i0.6
+qt.2 m0.4 dp.11.0 dp.9.0 dp.10.1 dv.9.0 fs.3.0 dv.11.0 dp.8.1 i0.4 xp.5.0 dv.8.1 dp.11.1 xp.5.1 dv.11.1 dp.10.0
+dv.10.0 dp.9.1 dv.9.1 dp.8.0 dv.8.0 tk.3 q0.4 ds.9 m0.5 xp.4.2 xp.0.2 xp.2.2 dv.10.1 q0.6 ds.11 i0.5 qt.3 m0.7
+dp.12.1 dp.12.0 dp.13.0 dv.13.0 i0.7 dv.12.1 dp.13.1 dv.13.1 dp.15.0 dv.15.0 dp.15.1 dv.15.1 dp.14.0 q0.5
+dp.14.1 ds.15 fs.3.1 dv.12.0 xp.5.2 xp.7.0 qf.3 ds.13 xp.7.1 q0.7 xp.0.3 xp.4.3 xs.0 dv.14.1 xp.7.2 xp.5.3 xs.4
+dv.14.0 xp.6.0 xp.2.3 xs.5 xp.6.1 ds.14 xp.7.3 xs.2 do.2 xp.1.0 xp.6.2 xs.7 xp.1.1 xp.6.3 xp.1.2 xs.6 xp.3.0
+xp.1.3 do.3 xp.3.1 xs.1 xp.3.2 do.0 xp.3.3 xs.3 do.1
 """
 
 
@@ -98,20 +98,29 @@ def tile_patchedsparsenetwork_pa_v_kernel(tc, x, W0, b0, m0, W1, b1, m1, pre0, p
             return sb("big", [P, 4 * 1024], BF16, NBIG)
 
         def lp(j):
-            live["pre1", j] = sb("outs", [P, D2], F32, NOUT)
-            nc.sync.dma_start(out=live["pre1", j][:], in_=pre1_v[:, j, :])
+            t = get(("pre1", j // 2), lambda: sb("outs", [P, 2, D2], F32, NOUT))
+            nc.sync.dma_start(out=t[:, j % 2], in_=pre1_v[:, j, :])
 
         def lg(j):
             grad = get("grad", big)
             nc.sync.dma_start(out=grad[:, part(j, D2)], in_=grad_v[:, j, :])
 
-        def lw(k):
-            t = get(("w1", k), lambda: sb("w1", [P, 2, T, HALF], BF16, 4))
-            nc.sync.dma_start(out=t[:, 0], in_=w1_v[k % NG, :, :, part(k // NG, HALF)])
+        chunk_of = {}
+        for i, width in enumerate(SPLIT):
+            for c in range(width):
+                chunk_of[sum(SPLIT[:i]) + c] = i, c
 
-        def lm(k):
-            t = get(("w1", k), lambda: sb("w1", [P, 2, T, HALF], BF16, 4))
-            nc.sync.dma_start(out=t[:, 1], in_=m1_v[k % NG, :, :, part(k // NG, HALF)])
+        def lw(i, g):
+            width = SPLIT[i]
+            cols = slice(sum(SPLIT[:i]) * HALF, sum(SPLIT[:i + 1]) * HALF)
+            live["w1", i, g] = sb("w1_" + str(width), [P, T, width * HALF], BF16, 2)
+            nc.sync.dma_start(out=live["w1", i, g][:], in_=w1_v[g, :, :, cols])
+
+        def lm(i, g):
+            width = SPLIT[i]
+            cols = slice(sum(SPLIT[:i]) * HALF, sum(SPLIT[:i + 1]) * HALF)
+            live["mm1", i, g] = sb("m1_" + str(width), [P, T, width * HALF], BF16, 2)
+            nc.sync.dma_start(out=live["mm1", i, g][:], in_=m1_v[g, :, :, cols])
 
         def l0(c):
             live["pre0", c] = sb("big", [P, T, HALF], F32, NBIG)
@@ -131,7 +140,7 @@ def tile_patchedsparsenetwork_pa_v_kernel(tc, x, W0, b0, m0, W1, b1, m1, pre0, p
 
         def dzV(j):
             live["dz2", j] = sb("dz2", [P, D2], BF16, 2)
-            nc.vector.scalar_tensor_tensor(out=live["dz2", j][:], in0=live["pre1", j][:], scalar=0.0,
+            nc.vector.scalar_tensor_tensor(out=live["dz2", j][:], in0=live["pre1", j // 2][:, j % 2], scalar=0.0,
                                            in1=live["grad"][:, part(j, D2)], op0=GT, op1=MULT)
 
         def dzT(j):
@@ -151,28 +160,27 @@ def tile_patchedsparsenetwork_pa_v_kernel(tc, x, W0, b0, m0, W1, b1, m1, pre0, p
                                   in_=live["dz2g"][:, g].rearrange("p j m t -> p (j m t)"))
 
         def mask_mult(a, b):
-            prod = sb("prod", [P, T, HALF], BF16, 3)
-            nc.vector.tensor_tensor(out=prod[:], in0=a, in1=b, op=MULT)
-            return prod
+            nc.vector.tensor_tensor(out=a, in0=a, in1=b, op=MULT)
+            return a
 
         def interleave(copy, src):
             grouped = sb("grouped", [P, HALF, T], BF16, 3)
-            copy(out=grouped[:], in_=src.rearrange("p t w -> p w t"))
+            copy(out=grouped[:].rearrange("p (c i) t -> p c t i", i=4), in_=src.rearrange("p t (c i) -> p c t i", i=4))
             return grouped
 
         def quant(codes, scales, grouped):
             nc.vector.quantize_mx(out=codes.bitcast(E4M3X4), scales=scales, in_=grouped[:].rearrange("p w t -> p (w t)"))
 
         def mul1(k):
-            t = live["w1", k]
-            live["pr", k] = mask_mult(t[:, 0], t[:, 1])
+            i, c = chunk_of[k // NG]
+            live["pr", k] = mask_mult(live["w1", i, k % NG][:, :, part(c, HALF)], live["mm1", i, k % NG][:, :, part(c, HALF)])
 
         def i1(k):
-            live["gr", k] = interleave(nc.scalar.copy, live["pr", k][:])
+            live["gr", k] = interleave(nc.vector.tensor_copy if k < 2 else nc.scalar.copy, live["pr", k])
 
         def q1(k):
-            codes = sb("w1c", [P, HALF], U32, 4)
-            scales = sb("w1s", [P, HALF], U8, 4)
+            codes = sb("w1c", [P, HALF], U32, 5)
+            scales = sb("w1s", [P, HALF], U8, 5)
             quant(codes[:], scales[:], live["gr", k])
             live["w1c", k] = codes, scales
 
@@ -203,7 +211,7 @@ def tile_patchedsparsenetwork_pa_v_kernel(tc, x, W0, b0, m0, W1, b1, m1, pre0, p
 
         def tk(c):
             live["tg", c] = sb("tokg", [P, T, P, T], BF16, 1)
-            nc.scalar.copy(out=live["tg", c][:], in_=live["dz1", c][:].rearrange("p t (m c) -> p c m t", c=T))
+            nc.scalar.copy(out=live["tg", c][:].rearrange("p c m t -> p m t c"), in_=live["dz1", c][:].rearrange("p t (m c) -> p m t c", c=T))
 
         def qf(c):
             nc.vector.quantize_mx(out=dz1f_codes[:, part(c, B)].bitcast(E5M2X4), scales=dz1f_scales[:, part(c, B)],
@@ -214,7 +222,7 @@ def tile_patchedsparsenetwork_pa_v_kernel(tc, x, W0, b0, m0, W1, b1, m1, pre0, p
                                   in_=live["tg", c][:].rearrange("p c m t -> p (c m t)"))
 
         def xi(n):
-            live["xg", n] = interleave(nc.vector.tensor_copy if n < 1 else nc.scalar.copy, live["x"][:, :, part(n, HALF)])
+            live["xg", n] = interleave(nc.vector.tensor_copy, live["x"][:, :, part(n, HALF)])
 
         def xq(n):
             quant(x_codes[:, part(n, HALF)], x_scales[:, part(n, HALF)], live["xg", n])
@@ -224,7 +232,7 @@ def tile_patchedsparsenetwork_pa_v_kernel(tc, x, W0, b0, m0, W1, b1, m1, pre0, p
             live["p0", i] = mask_mult(live["w0", q][:, :, part(n, HALF)], live["m0", q][:, :, part(n, HALF)])
 
         def i0(i):
-            live["g0", i] = interleave(nc.scalar.copy, live["p0", i][:])
+            live["g0", i] = interleave(nc.scalar.copy, live["p0", i])
 
         def q0(i):
             quant(w0_codes[:, part(i, HALF)], w0_scales[:, part(i, HALF)], live["g0", i])
@@ -237,11 +245,15 @@ def tile_patchedsparsenetwork_pa_v_kernel(tc, x, W0, b0, m0, W1, b1, m1, pre0, p
                                 rhs=x_codes[:, cols].bitcast(E4M3X4), rhs_scale=x_scales[:, cols], start=True, stop=True)
 
         def dv(i, n):
-            st = get(("st", i), lambda: sb("outs", [P, D0], F32, NOUT))
-            nc.vector.tensor_tensor(out=st[:, part(n, HALF)], in0=live["dwb", i, n][:], in1=live["m0", i // T][:, i % T, part(n, HALF)], op=MULT)
+            st = get(("st", i // 2), lambda: sb("outs", [P, 2, D0], F32, NOUT))
+            nc.vector.tensor_tensor(out=st[:, i % 2, part(n, HALF)], in0=live["dwb", i, n][:], in1=live["m0", i // T][:, i % T, part(n, HALF)], op=MULT)
 
         def ds(i):
-            nc.sync.dma_start(out=out1_v[i // T, :, i % T, :], in_=live["st", i][:])
+            st = live["st", i // 2]
+            if i >= 14:
+                nc.sync.dma_start(out=out1_v[i // T, :, i % T, :], in_=st[:, i % 2])
+            else:
+                nc.sync.dma_start(out=out1_v[i // T, :, i % T - 1:i % T + 1, :], in_=st[:])
 
         def xp(b, r):
             j, n = b // 2, b % 2
@@ -254,11 +266,11 @@ def tile_patchedsparsenetwork_pa_v_kernel(tc, x, W0, b0, m0, W1, b1, m1, pre0, p
                                 rhs=w0_codes[:, cols].bitcast(E4M3X4), rhs_scale=w0_scales[:, cols], start=(r == 0), stop=(r == NQ - 1))
 
         def xs(b):
-            st = get(("dst", b // 2), lambda: sb("outs", [P, D0], F32, NOUT))
-            nc.scalar.copy(out=st[:, part(b % 2, HALF)], in_=live["dxb", b][:])
+            st = get(("dst", b // 4), lambda: sb("outs", [P, 2, D0], F32, NOUT))
+            nc.scalar.copy(out=st[:, b // 2 % 2, part(b % 2, HALF)], in_=live["dxb", b][:])
 
         def do(j):
-            nc.sync.dma_start(out=out0_v[:, j, :], in_=live["dst", j][:])
+            nc.sync.dma_start(out=out0_v[:, j, :], in_=live["dst", j // 2][:, j % 2])
 
         pieces = {"lp": lp, "lg": lg, "lw": lw, "lm": lm, "l0": l0, "lM": lM, "lW": lW, "lx": lx, "dzV": dzV, "dzT": dzT, "dzS": dzS,
                   "qd": qd, "m1": mul1, "i1": i1, "q1": q1, "dh": dh, "mk": mk, "ft": ft, "fs": fs, "tk": tk, "qf": qf, "qt": qt,

@@ -23,27 +23,27 @@ K_PASS = P * T
 NQ = D1 // K_PASS
 NG = D2 // K_PASS
 HALF = 512
-SPLIT = (1, 3)
-NBIG = 6
+SPLIT = (2, 2)
+NBIG = 9
 NOUT = 4
 
 ORDER = """
-lg.0 lw.0.1 lm.0.1 lg.1 lp.1 lm.0.0 lw.0.0 lp.3 lg.2 lp.2 m1.1 lp.0 lg.3 i1.1 lx dzV.1 lW.0 q1.1 dzT.1 dzS.1
-m1.0 l0.0 lM.0 i1.0 lw.1.0 q1.0 lm.1.0 dzV.2 lm.1.1 dzV.0 dzT.2 lw.1.1 dzS.2 dzV.3 dzT.0 dzS.0 dzT.3 xi.1 l0.1
-dzS.3 qd.1 xq.1 qd.0 xi.0 dh.0.1 lM.1 dh.0.0 dh.0.3 xq.0 l0.2 mk.0.0 mk.0.3 dh.0.2 mk.0.1 mk.0.2 ft.0.0 m0.0
-tk.0 lW.1 ft.0.1 m0.1 i0.0 qt.0 dp.0.0 dp.3.0 dv.0.0 dp.0.1 dv.3.0 dp.1.0 dv.1.0 dp.3.1 i0.1 q0.0 dp.1.1 m1.4
-m1.2 i1.4 l0.3 m1.6 dv.3.1 dv.1.1 dp.2.1 i1.2 q1.4 dp.2.0 q0.1 dv.2.0 dv.0.1 i1.6 q1.2 ds.1 m1.3 m1.5 i1.3 m1.7
-q1.6 dv.2.1 i1.5 q1.3 ds.3 lW.3 dh.1.1 dh.1.0 mk.1.1 dh.1.3 mk.1.0 i1.7 dh.1.2 q1.5 mk.1.2 dh.2.0 mk.1.3 dh.2.2
-mk.2.0 lW.2 dh.2.3 mk.2.2 dh.2.1 fs.0.1 m0.2 fs.0.0 ft.1.1 tk.1 ft.1.0 q1.7 m0.3 dh.3.1 qf.0 mk.2.1 i0.3 mk.3.1
-dh.3.2 qt.1 dh.3.0 mk.2.3 dp.6.1 dp.6.0 dv.6.1 lM.3 dp.5.0 xp.4.0 dv.6.0 fs.1.1 dp.4.0 q0.3 dp.7.0 fs.1.0
-ft.2.0 dv.7.0 i0.2 ft.2.1 qf.1 mk.3.0 dp.5.1 dv.5.1 dh.3.3 dv.5.0 dp.4.1 fs.2.0 lM.2 q0.2 dp.7.1 tk.2 ft.3.0
-dv.7.1 xp.4.1 mk.3.3 ds.7 dv.4.1 xp.0.0 xp.0.1 mk.3.2 dv.4.0 xp.2.0 fs.2.1 xp.2.1 m0.6 ds.5 ft.3.1 qf.2 i0.6
-qt.2 m0.4 dp.11.0 dp.9.0 dp.10.1 dv.9.0 fs.3.0 dv.11.0 dp.8.1 i0.4 xp.5.0 dv.8.1 dp.11.1 xp.5.1 dv.11.1 dp.10.0
-dv.10.0 dp.9.1 dv.9.1 dp.8.0 dv.8.0 tk.3 q0.4 ds.9 m0.5 xp.4.2 xp.0.2 xp.2.2 dv.10.1 q0.6 ds.11 i0.5 qt.3 m0.7
-dp.12.1 dp.12.0 dp.13.0 dv.13.0 i0.7 dv.12.1 dp.13.1 dv.13.1 dp.15.0 dv.15.0 dp.15.1 dv.15.1 dp.14.0 q0.5
-dp.14.1 ds.15 fs.3.1 dv.12.0 xp.5.2 xp.7.0 qf.3 ds.13 xp.7.1 q0.7 xp.0.3 xp.4.3 xs.0 dv.14.1 xp.7.2 xp.5.3 xs.4
-dv.14.0 xp.6.0 xp.2.3 xs.5 xp.6.1 ds.14 xp.7.3 xs.2 do.2 xp.1.0 xp.6.2 xs.7 xp.1.1 xp.6.3 xp.1.2 xs.6 xp.3.0
-xp.1.3 do.3 xp.3.1 xs.1 xp.3.2 do.0 xp.3.3 xs.3 do.1
+lm.0.1 lw.0.1 lw.0.0 lm.0.0 lg.0 lg.3 lp.3 lp.0 lg.2 m1.0.1 lp.2 i1.1 lg.1 i1.3 q1.1 lp.1 m1.0.0 lx l0.0 q1.3
+l0.1 i1.0 dzV.3 lW.1 dzV.0 dzT.3 lM.1 i1.2 q1.0 dzT.0 lM.0 dzV.2 lw.1.0 dzV.1 lm.1.0 dzS.3 dzS.0 dzT.2 q1.2
+dzT.1 dzS.2 dzS.1 lm.1.1 xi.1 qd.0 qd.1 dh.0.2 dh.0.3 lw.1.1 mk.0.2 xi.0 dh.0.0 xq.1 dh.1.1 mk.0.0 mk.0.3
+dh.0.1 dh.1.3 mk.0.1 lW.2 ft.0.1 mk.1.1 tk.0 mk.1.3 dh.1.0 xq.0 dh.1.2 lM.2 mk.1.0 ft.0.0 mk.1.2 fs.0.0 qt.0
+fs.0.1 ft.1.0 m0.1 lW.0 tk.1 dp.0.1 dp.3.0 dp.1.0 ft.1.1 qf.0 l0.2 dv.1.0 dv.3.0 dp.1.1 fs.1.0 qt.1 dp.0.0
+fs.1.1 dv.1.1 i0.2 lM.3 qf.1 dp.4.0 dv.4.0 dv.0.1 dp.4.1 dv.4.1 dp.3.1 i0.3 lW.3 m1.1.0 dp.5.1 dv.3.1 i1.6 l0.3
+dv.5.1 dp.7.0 q0.2 dp.5.0 dv.5.0 q0.3 dp.2.1 i1.4 ds.5 q1.6 m1.1.1 q1.4 i1.7 dv.0.0 dv.2.1 dp.2.0 ds.1 dv.2.0
+dp.7.1 m0.2 dp.6.1 ds.3 i1.5 q1.7 i0.5 q1.5 dh.3.0 m0.0 dh.3.1 dh.2.0 i0.4 mk.2.0 q0.5 dh.2.2 dv.7.1 i0.1
+mk.2.2 dp.6.0 dv.6.0 dh.2.1 dv.7.0 mk.2.1 i0.0 m0.3 dh.2.3 ft.2.0 mk.2.3 fs.2.0 mk.3.1 dh.3.2 tk.2 mk.3.0
+ft.2.1 mk.3.2 dh.3.3 q0.1 ft.3.0 mk.3.3 q0.0 fs.2.1 qt.2 xp.6.0 xp.0.0 i0.6 qf.2 ft.3.1 dv.6.1 dp.8.0 dp.9.0
+dv.8.0 ds.7 dp.11.1 xp.6.1 dv.11.1 dp.9.1 fs.3.1 xp.0.1 dv.9.0 dp.11.0 fs.3.0 xp.2.0 dv.9.1 dp.8.1 tk.3 xp.2.1
+dv.11.0 dp.10.0 xp.3.0 dv.8.1 dp.10.1 xp.3.1 qf.3 ds.9 xp.1.0 xp.3.2 dv.10.0 xp.1.1 q0.4 xp.1.2 dv.10.1 i0.7
+xp.0.2 xp.6.2 qt.3 ds.11 xp.2.2 q0.6 dp.14.0 dp.15.1 dv.14.0 dp.14.1 xp.6.3 dv.14.1 xp.2.3 xs.6 dp.15.0 dv.15.1
+xp.0.3 ds.14 xs.2 dp.12.0 dv.15.0 dp.13.1 xs.0 xp.4.0 q0.7 ds.15 dp.13.0 xp.4.1 xp.3.3 xp.4.2 xs.3 dv.13.1
+xp.1.3 xp.4.3 xs.1 do.1 dv.13.0 dp.12.1 xp.7.0 xs.4 dv.12.1 do.0 xp.5.0 xp.7.1 dv.12.0 xp.5.1 xp.7.2 ds.13
+xp.5.2 xp.7.3 xp.5.3 xs.7 xs.5 do.3 do.2
 """
 
 
@@ -161,7 +161,6 @@ def tile_patchedsparsenetwork_pa_v_kernel(tc, x, W0, b0, m0, W1, b1, m1, pre0, p
 
         def mask_mult(a, b):
             nc.vector.tensor_tensor(out=a, in0=a, in1=b, op=MULT)
-            return a
 
         def interleave(copy, src):
             grouped = sb("grouped", [P, HALF, T], BF16, 3)
@@ -171,12 +170,11 @@ def tile_patchedsparsenetwork_pa_v_kernel(tc, x, W0, b0, m0, W1, b1, m1, pre0, p
         def quant(codes, scales, grouped):
             nc.vector.quantize_mx(out=codes.bitcast(E4M3X4), scales=scales, in_=grouped[:].rearrange("p w t -> p (w t)"))
 
-        def mul1(k):
-            i, c = chunk_of[k // NG]
-            live["pr", k] = mask_mult(live["w1", i, k % NG][:, :, part(c, HALF)], live["mm1", i, k % NG][:, :, part(c, HALF)])
+        def mul1(i, g):
+            mask_mult(live["w1", i, g][:], live["mm1", i, g][:])
 
         def i1(k):
-            live["gr", k] = interleave(nc.vector.tensor_copy if k < 2 else nc.scalar.copy, live["pr", k])
+            live["gr", k] = interleave(nc.scalar.copy, live["w1", chunk_of[k // NG][0], k % NG][:, :, part(chunk_of[k // NG][1], HALF)])
 
         def q1(k):
             codes = sb("w1c", [P, HALF], U32, 5)
@@ -222,17 +220,16 @@ def tile_patchedsparsenetwork_pa_v_kernel(tc, x, W0, b0, m0, W1, b1, m1, pre0, p
                                   in_=live["tg", c][:].rearrange("p c m t -> p (c m t)"))
 
         def xi(n):
-            live["xg", n] = interleave(nc.vector.tensor_copy, live["x"][:, :, part(n, HALF)])
+            live["xg", n] = interleave(nc.scalar.copy, live["x"][:, :, part(n, HALF)])
 
         def xq(n):
             quant(x_codes[:, part(n, HALF)], x_scales[:, part(n, HALF)], live["xg", n])
 
-        def mul0(i):
-            q, n = i // 2, i % 2
-            live["p0", i] = mask_mult(live["w0", q][:, :, part(n, HALF)], live["m0", q][:, :, part(n, HALF)])
+        def mul0(q):
+            mask_mult(live["w0", q][:], live["m0", q][:])
 
         def i0(i):
-            live["g0", i] = interleave(nc.scalar.copy, live["p0", i])
+            live["g0", i] = interleave(nc.scalar.copy, live["w0", i // 2][:, :, part(i % 2, HALF)])
 
         def q0(i):
             quant(w0_codes[:, part(i, HALF)], w0_scales[:, part(i, HALF)], live["g0", i])

@@ -5,7 +5,7 @@ from concourse.masks import make_identity
 
 B, D0, D1, D2 = 512, 1024, 2048, 1024
 
-FLOPS = 3 * 2 * B * D1 * max(D0, D2)
+FLOPS = 3 * 2 * B * D1 * D0
 BYTES = 2 * (B * D0 + 2 * D1 * D0 + 2 * D2 * D1 + B * D2) + 4 * (B * D1 + B * D2) + 4 * (B * D0 + D1 * D0)
 
 F32 = mybir.dt.float32
@@ -16,34 +16,42 @@ E4M3X4 = mybir.dt.float8_e4m3fn_x4
 E5M2X4 = mybir.dt.float8_e5m2_x4
 GT = mybir.AluOpType.is_gt
 MULT = mybir.AluOpType.mult
+ADD = mybir.AluOpType.add
 
 P = 128
 T = 4
 K_PASS = P * T
-NQ = D1 // K_PASS
-NG = D2 // K_PASS
-HALF = 512
-SPLIT = (2, 2)
-NBIG = 9
-NOUT = 4
+Q = D1 // K_PASS
+G = D2 // K_PASS
+N = 512
+H = 2
+LAST = 14
 
 ORDER = """
-lm.0.1 lw.0.1 lw.0.0 lm.0.0 lg.0 lg.3 lp.3 lp.0 lg.2 m1.0.1 lp.2 i1.1 lg.1 i1.3 q1.1 lp.1 m1.0.0 lx l0.0 q1.3
-l0.1 i1.0 dzV.3 lW.1 dzV.0 dzT.3 lM.1 i1.2 q1.0 dzT.0 lM.0 dzV.2 lw.1.0 dzV.1 lm.1.0 dzS.3 dzS.0 dzT.2 q1.2
-dzT.1 dzS.2 dzS.1 lm.1.1 xi.1 qd.0 qd.1 dh.0.2 dh.0.3 lw.1.1 mk.0.2 xi.0 dh.0.0 xq.1 dh.1.1 mk.0.0 mk.0.3
-dh.0.1 dh.1.3 mk.0.1 lW.2 ft.0.1 mk.1.1 tk.0 mk.1.3 dh.1.0 xq.0 dh.1.2 lM.2 mk.1.0 ft.0.0 mk.1.2 fs.0.0 qt.0
-fs.0.1 ft.1.0 m0.1 lW.0 tk.1 dp.0.1 dp.3.0 dp.1.0 ft.1.1 qf.0 l0.2 dv.1.0 dv.3.0 dp.1.1 fs.1.0 qt.1 dp.0.0
-fs.1.1 dv.1.1 i0.2 lM.3 qf.1 dp.4.0 dv.4.0 dv.0.1 dp.4.1 dv.4.1 dp.3.1 i0.3 lW.3 m1.1.0 dp.5.1 dv.3.1 i1.6 l0.3
-dv.5.1 dp.7.0 q0.2 dp.5.0 dv.5.0 q0.3 dp.2.1 i1.4 ds.5 q1.6 m1.1.1 q1.4 i1.7 dv.0.0 dv.2.1 dp.2.0 ds.1 dv.2.0
-dp.7.1 m0.2 dp.6.1 ds.3 i1.5 q1.7 i0.5 q1.5 dh.3.0 m0.0 dh.3.1 dh.2.0 i0.4 mk.2.0 q0.5 dh.2.2 dv.7.1 i0.1
-mk.2.2 dp.6.0 dv.6.0 dh.2.1 dv.7.0 mk.2.1 i0.0 m0.3 dh.2.3 ft.2.0 mk.2.3 fs.2.0 mk.3.1 dh.3.2 tk.2 mk.3.0
-ft.2.1 mk.3.2 dh.3.3 q0.1 ft.3.0 mk.3.3 q0.0 fs.2.1 qt.2 xp.6.0 xp.0.0 i0.6 qf.2 ft.3.1 dv.6.1 dp.8.0 dp.9.0
-dv.8.0 ds.7 dp.11.1 xp.6.1 dv.11.1 dp.9.1 fs.3.1 xp.0.1 dv.9.0 dp.11.0 fs.3.0 xp.2.0 dv.9.1 dp.8.1 tk.3 xp.2.1
-dv.11.0 dp.10.0 xp.3.0 dv.8.1 dp.10.1 xp.3.1 qf.3 ds.9 xp.1.0 xp.3.2 dv.10.0 xp.1.1 q0.4 xp.1.2 dv.10.1 i0.7
-xp.0.2 xp.6.2 qt.3 ds.11 xp.2.2 q0.6 dp.14.0 dp.15.1 dv.14.0 dp.14.1 xp.6.3 dv.14.1 xp.2.3 xs.6 dp.15.0 dv.15.1
-xp.0.3 ds.14 xs.2 dp.12.0 dv.15.0 dp.13.1 xs.0 xp.4.0 q0.7 ds.15 dp.13.0 xp.4.1 xp.3.3 xp.4.2 xs.3 dv.13.1
-xp.1.3 xp.4.3 xs.1 do.1 dv.13.0 dp.12.1 xp.7.0 xs.4 dv.12.1 do.0 xp.5.0 xp.7.1 dv.12.0 xp.5.1 xp.7.2 ds.13
-xp.5.2 xp.7.3 xp.5.3 xs.7 xs.5 do.3 do.2
+load_w1.0.0 load_m1.0.0 load_w1.0.1 load_m1.0.1 load_pre1.1 load_grad.1 load_grad.2 load_grad.3 load_pre1.3 w1_mask.0.0
+load_grad.0 w1_lay.2 load_pre1.0 w1_lay.0 w1_mask.0.1 load_pre1.2 load_pre0.0 load_x dz2_mask.1 w1_lay.1 load_pre0.1
+load_m1.1.0 w1_quant.0 dz2_turn.1 w1_quant.2 load_w1.1.0 dz2_mask.3 load_m0.0 dz2_lay.1 w1_lay.3 w1_quant.1 dz2_turn.3
+load_m1.1.1 dz2_mask.0 dz2_mask.2 dz2_turn.0 dz2_lay.3 load_w1.1.1 w1_quant.3 dz2_lay.0 dz2_turn.2 load_m0.1 dz2_lay.2
+dz2_quant.0 dz2_quant.1 x_lay.1 load_w0.1 dh.0.2 dh.0.1 dz1_mask.0.2 dh.0.0 dz1_mask.0.1 dh.0.3 dz1_mask.0.0 dh.1.1
+load_pre0.2 dz1_mask.0.3 x_lay.0 dh.1.3 dz1_mask.1.1 dz1t_lay.0 dh.1.0 dz1_mask.1.3 dh.1.2 dz1_mask.1.0 dz1_turn.0.0
+dz1_mask.1.2 load_w0.0 dz1_turn.0.1 x_quant.1 x_quant.0 dz1f_lay.0.1 dz1t_quant.0 dz1f_lay.0.0 load_m0.2 dz1_turn.1.1
+w1_mask.1.0 dz1t_lay.1 dw.0.1 dw.1.1 dw.2.1 dz1_turn.1.0 dz1f_quant.0 load_w0.2 dw_mask.0.1 dw_mask.1.1 dw.2.0 w1_lay.4
+dw_mask.2.1 dw.1.0 dw_mask.2.0 load_pre0.3 dw.0.0 dw_mask.1.0 dw.3.0 dw_mask.0.0 dw.3.1 w1_lay.6 dw_mask.3.0 w1_quant.4
+dw_store.1 dw_mask.3.1 w1_mask.1.1 dz1f_lay.1.0 dz1f_lay.1.1 dw_store.3 w1_quant.6 w1_lay.5 dz1t_quant.1 dz1f_quant.1
+dw.4.0 load_m0.3 dw.4.1 w0_mask.1 dw.5.0 w1_lay.7 dw_mask.5.0 dw_mask.4.0 dw.5.1 dw_mask.4.1 w0_lay.2 dw.7.1
+dw_mask.5.1 dw.6.1 dw_mask.7.1 dw.6.0 dw_store.5 w1_quant.5 dw.7.0 dw_mask.6.0 dh.2.1 w0_lay.3 dw_mask.7.0 dh.2.0
+dz1_mask.2.1 dh.2.2 dz1_mask.2.0 dh.2.3 dz1_mask.2.2 dz1_turn.2.0 dz1_mask.2.3 load_w0.3 w0_quant.3 dz1f_lay.2.0
+dz1_turn.2.1 w1_quant.7 dz1t_lay.2 dw_mask.6.1 dh.3.1 w0_quant.2 dw_store.7 dh.3.3 w0_mask.0 dh.3.2 dz1f_lay.2.1
+dz1_mask.3.1 w0_lay.1 dz1_mask.3.2 dh.3.0 dz1_mask.3.3 dz1_mask.3.0 dz1_turn.3.1 dz1t_quant.2 dz1_turn.3.0 w0_lay.0
+w0_mask.2 dw.10.1 dw.9.1 dw.11.0 dw_mask.11.0 dz1t_lay.3 w0_quant.0 dw.10.0 dw_mask.9.1 dx.6.0 dx.2.0 dw_mask.10.1
+dx.6.1 dx.4.0 w0_quant.1 dx.2.1 dx.4.1 dw_mask.10.0 dw.9.0 dw.11.1 dz1f_quant.2 w0_lay.4 dw.8.0 dw_mask.11.1
+dw_mask.9.0 dw.8.1 dw_store.11 dw_mask.8.0 w0_mask.3 dz1f_lay.3.1 dz1f_lay.3.0 dx.5.0 w0_lay.5 dx.5.1 dx.7.0 w0_quant.4
+dx.7.1 dw_mask.8.1 dx.4.2 dx.6.2 dz1t_quant.3 dw_store.9 dx.2.2 w0_lay.7 dz1f_quant.3 dw.13.1 dw.15.1 w0_quant.5
+dw.13.0 dw_mask.13.1 dx.5.2 dx.7.2 dw_mask.15.1 dw.15.0 dw_mask.13.0 w0_lay.6 dw.12.1 dw_mask.15.0 dw.12.0 dw_mask.12.1
+dw.14.0 dw_store.15 dw_mask.12.0 dw.14.1 w0_quant.7 dw_store.13 w0_quant.6 dx.5.3 dx.7.3 dw_mask.14.1 dx_copy.5 dx.6.3
+dx.2.3 dw_mask.14.0 dx_copy.7 dx.4.3 dx.3.0 dx_copy.6 dw_store.14 dx.1.0 dx.3.1 dx_copy.4 dx_store.3 dx.0.0 dx.3.2
+dx_copy.2 dx_store.2 dx.0.1 dx.3.3 dx.0.2 dx_copy.3 dx.1.1 dx.0.3 dx.1.2 dx_store.1 dx_copy.0 dx.1.3 dx_copy.1
+dx_store.0
 """
 
 
@@ -55,223 +63,228 @@ def tile_patchedsparsenetwork_pa_v_kernel(tc, x, W0, b0, m0, W1, b1, m1, pre0, p
         psum = ctx.enter_context(tc.psum_pool(name="psum", bufs=1))
         ctx.enter_context(tc.manual_schedule())
 
-        ident_f = keep.tile([P, P], F32, name="ident_f")
-        make_identity(nc, ident_f[:])
+        identity = keep.tile([P, P], F32, name="identity")
+        make_identity(nc, identity[:])
 
-        def plane(width, nm, dtype):
-            return keep.tile([P, width], dtype, name=nm, align_bytes=64)
+        def quantised(width, name):
+            return (keep.tile([P, width], U32, name=name + "_codes", align_bytes=64),
+                    keep.tile([P, width], U8, name=name + "_scales", align_bytes=64))
 
-        dz2_codes, dz2_scales = plane(NG * B, "dz2_codes", U32), plane(NG * B, "dz2_scales", U8)
-        dz1f_codes, dz1f_scales = plane(NQ * B, "dz1f_codes", U32), plane(NQ * B, "dz1f_scales", U8)
-        dz1t_codes, dz1t_scales = plane(D1, "dz1t_codes", U32), plane(D1, "dz1t_scales", U8)
-        x_codes, x_scales = plane(D0, "x_codes", U32), plane(D0, "x_scales", U8)
-        w0_codes, w0_scales = plane(NQ * D0, "w0_codes", U32), plane(NQ * D0, "w0_scales", U8)
+        dz2_q = quantised(G * B, "dz2")
+        dz1f_q = quantised(Q * B, "dz1f")
+        dz1t_q = quantised(D1, "dz1t")
+        x_q = quantised(D0, "x")
+        w0_q = quantised(Q * D0, "w0")
 
-        pre1_v = pre1.rearrange("(p j) w -> p j w", j=T)
-        grad_v = grad_out.rearrange("(p j) w -> p j w", j=T)
-        pre0_v = pre0.rearrange("(p j) w -> p j w", j=T)
-        x_v = x.rearrange("(p j) w -> p j w", j=T)
-        w1_v = W1.rearrange("(g p j) w -> g p j w", p=P, j=T)
-        m1_v = m1.rearrange("(g p j) w -> g p j w", p=P, j=T)
-        w0_v = W0.rearrange("(g p j) w -> g p j w", p=P, j=T)
-        m0_v = m0.rearrange("(g p j) w -> g p j w", p=P, j=T)
-        out0_v = out_0.rearrange("(p j) w -> p j w", j=T)
-        out1_v = out_1.rearrange("(g p j) w -> g p j w", p=P, j=T)
+        by_token = "(p j) w -> p j w"
+        by_pass = "(g p j) w -> g p j w"
+        pre1_v, grad_v, pre0_v, x_v, out0_v = (a.rearrange(by_token, j=T) for a in (pre1, grad_out, pre0, x, out_0))
+        w1_v, m1_v, w0_v, m0_v, out1_v = (a.rearrange(by_pass, p=P, j=T) for a in (W1, m1, W0, m0, out_1))
 
         live = {}
 
         def part(i, width):
             return slice(i * width, (i + 1) * width)
 
-        def get(key, make):
+        def kept(key, make):
             if key not in live:
                 live[key] = make()
             return live[key]
 
-        def sb(tag, shape, dtype, bufs):
+        def sbuf(tag, shape, dtype, bufs):
             return work.tile(shape, dtype, name=tag, tag=tag, bufs=bufs, align_bytes=64)
 
-        def ps(tag, shape, dtype, bufs):
-            return psum.tile(shape, dtype, name=tag, tag=tag, bufs=bufs)
+        def bank(tag, shape, bufs):
+            return psum.tile(shape, F32, name=tag, tag=tag, bufs=bufs)
 
-        def big():
-            return sb("big", [P, 4 * 1024], BF16, NBIG)
+        def big(shape, dtype=BF16):
+            return sbuf("big", shape, dtype, 9)
 
-        def lp(j):
-            t = get(("pre1", j // 2), lambda: sb("outs", [P, 2, D2], F32, NOUT))
-            nc.sync.dma_start(out=t[:, j % 2], in_=pre1_v[:, j, :])
+        def outs():
+            return sbuf("outs", [P, 2, D0], F32, 4)
 
-        def lg(j):
-            grad = get("grad", big)
-            nc.sync.dma_start(out=grad[:, part(j, D2)], in_=grad_v[:, j, :])
+        def grouped():
+            return sbuf("grouped", [P, N, T], BF16, 4)
 
-        chunk_of = {}
-        for i, width in enumerate(SPLIT):
-            for c in range(width):
-                chunk_of[sum(SPLIT[:i]) + c] = i, c
+        def turned(tag):
+            return bank(tag, [P, 2, 2, P], 2)
 
-        def lw(i, g):
-            width = SPLIT[i]
-            cols = slice(sum(SPLIT[:i]) * HALF, sum(SPLIT[:i + 1]) * HALF)
-            live["w1", i, g] = sb("w1_" + str(width), [P, T, width * HALF], BF16, 2)
-            nc.sync.dma_start(out=live["w1", i, g][:], in_=w1_v[g, :, :, cols])
+        def load_pre1(j):
+            rows = kept(("pre1", j // 2), outs)
+            nc.sync.dma_start(out=rows[:, j % 2], in_=pre1_v[:, j, :])
 
-        def lm(i, g):
-            width = SPLIT[i]
-            cols = slice(sum(SPLIT[:i]) * HALF, sum(SPLIT[:i + 1]) * HALF)
-            live["mm1", i, g] = sb("m1_" + str(width), [P, T, width * HALF], BF16, 2)
-            nc.sync.dma_start(out=live["mm1", i, g][:], in_=m1_v[g, :, :, cols])
+        def load_grad(j):
+            rows = kept("grad", lambda: big([P, T * D2]))
+            nc.sync.dma_start(out=rows[:, part(j, D2)], in_=grad_v[:, j, :])
 
-        def l0(c):
-            live["pre0", c] = sb("big", [P, T, HALF], F32, NBIG)
-            nc.sync.dma_start(out=live["pre0", c][:], in_=pre0_v[:, :, part(c, HALF)])
+        def load_half(name, src, h, g):
+            live[name, h, g] = sbuf(name + "_2", [P, T, H * N], BF16, 2)
+            nc.sync.dma_start(out=live[name, h, g][:], in_=src[g, :, :, part(h, H * N)])
 
-        def lM(c):
-            live["m0", c] = sb("big", [P, T, D0], BF16, NBIG)
-            nc.sync.dma_start(out=live["m0", c][:], in_=m0_v[c])
+        def load_w1(h, g):
+            load_half("w1", w1_v, h, g)
 
-        def lW(c):
-            live["w0", c] = sb("big", [P, T, D0], BF16, NBIG)
-            nc.sync.dma_start(out=live["w0", c][:], in_=w0_v[c])
+        def load_m1(h, g):
+            load_half("m1", m1_v, h, g)
 
-        def lx():
-            live["x"] = sb("big", [P, T, D0], BF16, NBIG)
+        def load_pre0(q):
+            live["pre0", q] = big([P, T, N], F32)
+            nc.sync.dma_start(out=live["pre0", q][:], in_=pre0_v[:, :, part(q, N)])
+
+        def load_m0(q):
+            live["m0", q] = big([P, T, D0])
+            nc.sync.dma_start(out=live["m0", q][:], in_=m0_v[q])
+
+        def load_w0(q):
+            live["w0", q] = big([P, T, D0])
+            nc.sync.dma_start(out=live["w0", q][:], in_=w0_v[q])
+
+        def load_x():
+            live["x"] = big([P, T, D0])
             nc.sync.dma_start(out=live["x"][:], in_=x_v)
 
-        def dzV(j):
-            live["dz2", j] = sb("dz2", [P, D2], BF16, 2)
+        def turn(words, where):
+            for u in range(2):
+                nc.tensor.transpose(where[:, u, :], words[:, u:2 * P:2], identity[:])
+
+        def lay(rows):
+            tile = grouped()
+            nc.scalar.copy(out=tile[:].rearrange("p (c i) t -> p c t i", i=4), in_=rows.rearrange("p t (c i) -> p c t i", i=4))
+            return tile
+
+        def lay_on_gpsimd(rows):
+            tile = grouped()
+            nc.gpsimd.tensor_scalar(out=tile[:], in0=rows.rearrange("p t w -> p w t"), scalar1=1.0, scalar2=0.0, op0=MULT, op1=ADD)
+            return tile
+
+        def quantise(planes, cols, words, fmt):
+            codes, scales = planes
+            nc.vector.quantize_mx(out=codes[:, cols].bitcast(fmt), scales=scales[:, cols], in_=words)
+
+        def product(out, left, left_cols, right, right_cols, first, last):
+            (lc, ls), (rc, rs) = left, right
+            nc.tensor.matmul_mx(out=out[:], lhsT=lc[:, left_cols].bitcast(E5M2X4), lhsT_scale=ls[:, left_cols],
+                                rhs=rc[:, right_cols].bitcast(E4M3X4), rhs_scale=rs[:, right_cols], start=first, stop=last)
+
+        def dz2_mask(j):
+            live["dz2", j] = sbuf("dz2", [P, D2], BF16, 2)
             nc.vector.scalar_tensor_tensor(out=live["dz2", j][:], in0=live["pre1", j // 2][:, j % 2], scalar=0.0,
                                            in1=live["grad"][:, part(j, D2)], op0=GT, op1=MULT)
 
-        def dzT(j):
-            bank = ps("tp", [P, NG, 2, P], F32, 2)
-            live["dzb", j] = bank
+        def dz2_turn(j):
+            live["dz2_t", j] = turned("turned")
             words = live["dz2", j][:].bitcast(F32)
-            for g in range(NG):
-                for u in range(2):
-                    nc.tensor.transpose(bank[:, g, u, :], words[:, 256 * g + u:256 * (g + 1):2], ident_f[:])
+            for g in range(G):
+                turn(words[:, part(g, 2 * P)], live["dz2_t", j][:, g])
 
-        def dzS(j):
-            grouped = get("dz2g", lambda: sb("big", [P, NG, T, P, T], BF16, NBIG))
-            nc.scalar.copy(out=grouped[:, :, j].bitcast(F32), in_=live["dzb", j][:].rearrange("p g u m -> p g m u"))
+        def dz2_lay(j):
+            tile = kept("dz2_g", lambda: big([P, G, T, P, T]))
+            nc.scalar.copy(out=tile[:, :, j].bitcast(F32), in_=live["dz2_t", j][:].rearrange("p g u m -> p g m u"))
 
-        def qd(g):
-            nc.vector.quantize_mx(out=dz2_codes[:, part(g, B)].bitcast(E5M2X4), scales=dz2_scales[:, part(g, B)],
-                                  in_=live["dz2g"][:, g].rearrange("p j m t -> p (j m t)"))
+        def dz2_quant(g):
+            quantise(dz2_q, part(g, B), live["dz2_g"][:, g].rearrange("p j m t -> p (j m t)"), E5M2X4)
 
-        def mask_mult(a, b):
-            nc.vector.tensor_tensor(out=a, in0=a, in1=b, op=MULT)
+        def w1_mask(h, g):
+            w = live["w1", h, g]
+            nc.vector.tensor_tensor(out=w[:], in0=w[:], in1=live["m1", h, g][:], op=MULT)
 
-        def interleave(copy, src):
-            grouped = sb("grouped", [P, HALF, T], BF16, 3)
-            copy(out=grouped[:].rearrange("p (c i) t -> p c t i", i=4), in_=src.rearrange("p t (c i) -> p c t i", i=4))
-            return grouped
+        def w1_lay(k):
+            q, g = k // G, k % G
+            live["w1_g", k] = lay(live["w1", q // H, g][:, :, part(q % H, N)])
 
-        def quant(codes, scales, grouped):
-            nc.vector.quantize_mx(out=codes.bitcast(E4M3X4), scales=scales, in_=grouped[:].rearrange("p w t -> p (w t)"))
+        def w1_quant(k):
+            live["w1_q", k] = (sbuf("w1_codes", [P, N], U32, 5), sbuf("w1_scales", [P, N], U8, 5))
+            quantise(live["w1_q", k], slice(0, N), live["w1_g", k][:].rearrange("p w t -> p (w t)"), E4M3X4)
 
-        def mul1(i, g):
-            mask_mult(live["w1", i, g][:], live["mm1", i, g][:])
+        def dh(q, j):
+            live["dh", q, j] = bank("dh", [P, N], 3)
+            for g in range(G):
+                product(live["dh", q, j], dz2_q, slice(g * B + j * P, g * B + (j + 1) * P), live["w1_q", G * q + g], slice(0, N),
+                        g == 0, g == G - 1)
 
-        def i1(k):
-            live["gr", k] = interleave(nc.scalar.copy, live["w1", chunk_of[k // NG][0], k % NG][:, :, part(chunk_of[k // NG][1], HALF)])
+        def dz1_mask(q, j):
+            tile = kept(("dz1", q), lambda: sbuf("dz1", [P, T, N], BF16, 2))
+            nc.vector.scalar_tensor_tensor(out=tile[:, j], in0=live["pre0", q][:, j], scalar=0.0, in1=live["dh", q, j][:],
+                                           op0=GT, op1=MULT)
 
-        def q1(k):
-            codes = sb("w1c", [P, HALF], U32, 5)
-            scales = sb("w1s", [P, HALF], U8, 5)
-            quant(codes[:], scales[:], live["gr", k])
-            live["w1c", k] = codes, scales
+        def dz1_turn(q, pair):
+            live["dz1_t", q, pair] = turned("turned")
+            for i in range(2):
+                turn(live["dz1", q][:, 2 * pair + i].bitcast(F32), live["dz1_t", q, pair][:, i])
 
-        def dh(c, j):
-            bank = ps("dh", [P, HALF], F32, 3)
-            live["dhb", c, j] = bank
-            for g in range(NG):
-                codes, scales = live["w1c", NG * c + g]
-                cols = slice(g * B + j * P, g * B + (j + 1) * P)
-                nc.tensor.matmul_mx(out=bank[:], lhsT=dz2_codes[:, cols].bitcast(E5M2X4), lhsT_scale=dz2_scales[:, cols],
-                                    rhs=codes[:].bitcast(E4M3X4), rhs_scale=scales[:], start=(g == 0), stop=(g == NG - 1))
+        def dz1f_lay(q, pair):
+            tile = kept(("dz1f_g", q), lambda: sbuf("dz1f_g", [P, T, P, T], BF16, 1))
+            nc.scalar.copy(out=tile[:, part(pair, 2)].bitcast(F32),
+                           in_=live["dz1_t", q, pair][:].rearrange("p j u m -> p j m u"))
 
-        def mk(c, j):
-            dz1 = get(("dz1", c), lambda: sb("dz1", [P, T, HALF], BF16, 2))
-            nc.vector.scalar_tensor_tensor(out=dz1[:, j], in0=live["pre0", c][:, j], scalar=0.0, in1=live["dhb", c, j][:], op0=GT, op1=MULT)
+        def dz1f_quant(q):
+            quantise(dz1f_q, part(q, B), live["dz1f_g", q][:].rearrange("p j m t -> p (j m t)"), E5M2X4)
 
-        def ft(c, h):
-            bank = ps("tp", [P, 2, 2, P], F32, 2)
-            live["fb", c, h] = bank
-            for jl in range(2):
-                words = live["dz1", c][:, 2 * h + jl].bitcast(F32)
-                for u in range(2):
-                    nc.tensor.transpose(bank[:, jl, u, :], words[:, u:256:2], ident_f[:])
+        def dz1t_lay(q):
+            live["dz1t_g", q] = sbuf("dz1t_g", [P, T, P, T], BF16, 1)
+            nc.scalar.copy(out=live["dz1t_g", q][:].rearrange("p c m t -> p m t c"),
+                           in_=live["dz1", q][:].rearrange("p t (m c) -> p m t c", c=T))
 
-        def fs(c, h):
-            grouped = get(("fg", c), lambda: sb("featg", [P, T, P, T], BF16, 1))
-            nc.scalar.copy(out=grouped[:, 2 * h:2 * h + 2].bitcast(F32), in_=live["fb", c, h][:].rearrange("p j u m -> p j m u"))
+        def dz1t_quant(q):
+            quantise(dz1t_q, part(q, N), live["dz1t_g", q][:].rearrange("p c m t -> p (c m t)"), E5M2X4)
 
-        def tk(c):
-            live["tg", c] = sb("tokg", [P, T, P, T], BF16, 1)
-            nc.scalar.copy(out=live["tg", c][:].rearrange("p c m t -> p m t c"), in_=live["dz1", c][:].rearrange("p t (m c) -> p m t c", c=T))
+        def x_lay(n):
+            live["x_g", n] = lay_on_gpsimd(live["x"][:, :, part(n, N)])
 
-        def qf(c):
-            nc.vector.quantize_mx(out=dz1f_codes[:, part(c, B)].bitcast(E5M2X4), scales=dz1f_scales[:, part(c, B)],
-                                  in_=live["fg", c][:].rearrange("p j m t -> p (j m t)"))
+        def x_quant(n):
+            quantise(x_q, part(n, N), live["x_g", n][:].rearrange("p w t -> p (w t)"), E4M3X4)
 
-        def qt(c):
-            nc.vector.quantize_mx(out=dz1t_codes[:, part(c, HALF)].bitcast(E5M2X4), scales=dz1t_scales[:, part(c, HALF)],
-                                  in_=live["tg", c][:].rearrange("p c m t -> p (c m t)"))
+        def w0_mask(q):
+            w = live["w0", q]
+            nc.vector.tensor_tensor(out=w[:], in0=w[:], in1=live["m0", q][:], op=MULT)
 
-        def xi(n):
-            live["xg", n] = interleave(nc.scalar.copy, live["x"][:, :, part(n, HALF)])
+        def w0_lay(i):
+            live["w0_g", i] = lay(live["w0", i // 2][:, :, part(i % 2, N)])
 
-        def xq(n):
-            quant(x_codes[:, part(n, HALF)], x_scales[:, part(n, HALF)], live["xg", n])
+        def w0_quant(i):
+            quantise(w0_q, part(i, N), live["w0_g", i][:].rearrange("p w t -> p (w t)"), E4M3X4)
 
-        def mul0(q):
-            mask_mult(live["w0", q][:], live["m0", q][:])
+        def dw(i, n):
+            live["dw", i, n] = bank("dw", [P, N], 3)
+            product(live["dw", i, n], dz1t_q, part(i, P), x_q, part(n, N), True, True)
 
-        def i0(i):
-            live["g0", i] = interleave(nc.scalar.copy, live["w0", i // 2][:, :, part(i % 2, HALF)])
+        def dw_mask(i, n):
+            rows = kept(("dw_out", i // 2), outs)
+            nc.vector.tensor_tensor(out=rows[:, i % 2, part(n, N)], in0=live["dw", i, n][:],
+                                    in1=live["m0", i // T][:, i % T, part(n, N)], op=MULT)
 
-        def q0(i):
-            quant(w0_codes[:, part(i, HALF)], w0_scales[:, part(i, HALF)], live["g0", i])
-
-        def dp(i, n):
-            bank = ps("dw", [P, HALF], F32, 3)
-            live["dwb", i, n] = bank
-            rows, cols = part(i, P), part(n, HALF)
-            nc.tensor.matmul_mx(out=bank[:], lhsT=dz1t_codes[:, rows].bitcast(E5M2X4), lhsT_scale=dz1t_scales[:, rows],
-                                rhs=x_codes[:, cols].bitcast(E4M3X4), rhs_scale=x_scales[:, cols], start=True, stop=True)
-
-        def dv(i, n):
-            st = get(("st", i // 2), lambda: sb("outs", [P, 2, D0], F32, NOUT))
-            nc.vector.tensor_tensor(out=st[:, i % 2, part(n, HALF)], in0=live["dwb", i, n][:], in1=live["m0", i // T][:, i % T, part(n, HALF)], op=MULT)
-
-        def ds(i):
-            st = live["st", i // 2]
-            if i >= 14:
-                nc.sync.dma_start(out=out1_v[i // T, :, i % T, :], in_=st[:, i % 2])
+        def dw_store(i):
+            q, c = i // T, i % T
+            rows = live["dw_out", i // 2]
+            if i >= LAST:
+                nc.sync.dma_start(out=out1_v[q, :, c, :], in_=rows[:, i % 2])
             else:
-                nc.sync.dma_start(out=out1_v[i // T, :, i % T - 1:i % T + 1, :], in_=st[:])
+                nc.sync.dma_start(out=out1_v[q, :, c - 1:c + 1, :], in_=rows[:])
 
-        def xp(b, r):
+        def dx(b, q):
             j, n = b // 2, b % 2
-            if r == 0:
-                tag, bufs = ("tp", 2) if b in (1, 3, 5, 7) else ("dh", 3)
-                live["dxb", b] = ps(tag, [P, HALF], F32, bufs)
-            rows = slice(r * B + j * P, r * B + (j + 1) * P)
-            cols = slice(r * D0 + n * HALF, r * D0 + (n + 1) * HALF)
-            nc.tensor.matmul_mx(out=live["dxb", b][:], lhsT=dz1f_codes[:, rows].bitcast(E5M2X4), lhsT_scale=dz1f_scales[:, rows],
-                                rhs=w0_codes[:, cols].bitcast(E4M3X4), rhs_scale=w0_scales[:, cols], start=(r == 0), stop=(r == NQ - 1))
+            if q == 0:
+                live["dx", b] = bank("turned", [P, N], 2) if n else bank("dh", [P, N], 3)
+            product(live["dx", b], dz1f_q, slice(q * B + j * P, q * B + (j + 1) * P), w0_q, slice(q * D0 + n * N, q * D0 + (n + 1) * N),
+                    q == 0, q == Q - 1)
 
-        def xs(b):
-            st = get(("dst", b // 4), lambda: sb("outs", [P, 2, D0], F32, NOUT))
-            nc.scalar.copy(out=st[:, b // 2 % 2, part(b % 2, HALF)], in_=live["dxb", b][:])
+        def dx_copy(b):
+            rows = kept(("dx_out", b // 4), outs)
+            nc.scalar.copy(out=rows[:, b // 2 % 2, part(b % 2, N)], in_=live["dx", b][:])
 
-        def do(j):
-            nc.sync.dma_start(out=out0_v[:, j, :], in_=live["dst", j // 2][:, j % 2])
+        def dx_store(j):
+            nc.sync.dma_start(out=out0_v[:, j, :], in_=live["dx_out", j // 2][:, j % 2])
 
-        pieces = {"lp": lp, "lg": lg, "lw": lw, "lm": lm, "l0": l0, "lM": lM, "lW": lW, "lx": lx, "dzV": dzV, "dzT": dzT, "dzS": dzS,
-                  "qd": qd, "m1": mul1, "i1": i1, "q1": q1, "dh": dh, "mk": mk, "ft": ft, "fs": fs, "tk": tk, "qf": qf, "qt": qt,
-                  "xi": xi, "xq": xq, "m0": mul0, "i0": i0, "q0": q0, "dp": dp, "dv": dv, "ds": ds, "xp": xp, "xs": xs, "do": do}
+        steps = {
+            "load_pre1": load_pre1, "load_grad": load_grad, "load_w1": load_w1, "load_m1": load_m1, "load_pre0": load_pre0,
+            "load_m0": load_m0, "load_w0": load_w0, "load_x": load_x,
+            "dz2_mask": dz2_mask, "dz2_turn": dz2_turn, "dz2_lay": dz2_lay, "dz2_quant": dz2_quant,
+            "w1_mask": w1_mask, "w1_lay": w1_lay, "w1_quant": w1_quant,
+            "dh": dh, "dz1_mask": dz1_mask, "dz1_turn": dz1_turn, "dz1f_lay": dz1f_lay, "dz1f_quant": dz1f_quant,
+            "dz1t_lay": dz1t_lay, "dz1t_quant": dz1t_quant,
+            "x_lay": x_lay, "x_quant": x_quant, "w0_mask": w0_mask, "w0_lay": w0_lay, "w0_quant": w0_quant,
+            "dw": dw, "dw_mask": dw_mask, "dw_store": dw_store, "dx": dx, "dx_copy": dx_copy, "dx_store": dx_store,
+        }
         for word in ORDER.split():
-            parts = word.split(".")
-            pieces[parts[0]](*[int(a) for a in parts[1:]])
+            step = word.split(".")
+            steps[step[0]](*[int(index) for index in step[1:]])

from contextlib import ExitStack

import concourse.mybir as mybir
from concourse.masks import make_identity

B, D0, D1, D2 = 512, 1024, 2048, 1024

FLOPS = 3 * 2 * B * D1 * D0
BYTES = 2 * (B * D0 + 2 * D1 * D0 + 2 * D2 * D1 + B * D2) + 4 * (B * D1 + B * D2) + 4 * (B * D0 + D1 * D0)

F32 = mybir.dt.float32
BF16 = mybir.dt.bfloat16
U32 = mybir.dt.uint32
U8 = mybir.dt.uint8
E4M3X4 = mybir.dt.float8_e4m3fn_x4
E5M2X4 = mybir.dt.float8_e5m2_x4
GT = mybir.AluOpType.is_gt
MULT = mybir.AluOpType.mult
ADD = mybir.AluOpType.add

P = 128
T = 4
K_PASS = P * T
Q = D1 // K_PASS
G = D2 // K_PASS
N = 512
H = 2
LAST = 14

ORDER = """
load_w1.0.0 load_m1.0.0 load_w1.0.1 load_m1.0.1 load_pre1.1 load_grad.1 load_grad.2 load_grad.3 load_pre1.3 w1_mask.0.0
load_grad.0 w1_lay.2 load_pre1.0 w1_lay.0 w1_mask.0.1 load_pre1.2 load_pre0.0 load_x dz2_mask.1 w1_lay.1 load_pre0.1
load_m1.1.0 w1_quant.0 dz2_turn.1 w1_quant.2 load_w1.1.0 dz2_mask.3 load_m0.0 dz2_lay.1 w1_lay.3 w1_quant.1 dz2_turn.3
load_m1.1.1 dz2_mask.0 dz2_mask.2 dz2_turn.0 dz2_lay.3 load_w1.1.1 w1_quant.3 dz2_lay.0 dz2_turn.2 load_m0.1 dz2_lay.2
dz2_quant.0 dz2_quant.1 x_lay.1 load_w0.1 dh.0.2 dh.0.1 dz1_mask.0.2 dh.0.0 dz1_mask.0.1 dh.0.3 dz1_mask.0.0 dh.1.1
load_pre0.2 dz1_mask.0.3 x_lay.0 dh.1.3 dz1_mask.1.1 dz1t_lay.0 dh.1.0 dz1_mask.1.3 dh.1.2 dz1_mask.1.0 dz1_turn.0.0
dz1_mask.1.2 load_w0.0 dz1_turn.0.1 x_quant.1 x_quant.0 dz1f_lay.0.1 dz1t_quant.0 dz1f_lay.0.0 load_m0.2 dz1_turn.1.1
w1_mask.1.0 dz1t_lay.1 dw.0.1 dw.1.1 dw.2.1 dz1_turn.1.0 dz1f_quant.0 load_w0.2 dw_mask.0.1 dw_mask.1.1 dw.2.0 w1_lay.4
dw_mask.2.1 dw.1.0 dw_mask.2.0 load_pre0.3 dw.0.0 dw_mask.1.0 dw.3.0 dw_mask.0.0 dw.3.1 w1_lay.6 dw_mask.3.0 w1_quant.4
dw_store.1 dw_mask.3.1 w1_mask.1.1 dz1f_lay.1.0 dz1f_lay.1.1 dw_store.3 w1_quant.6 w1_lay.5 dz1t_quant.1 dz1f_quant.1
dw.4.0 load_m0.3 dw.4.1 w0_mask.1 dw.5.0 w1_lay.7 dw_mask.5.0 dw_mask.4.0 dw.5.1 dw_mask.4.1 w0_lay.2 dw.7.1
dw_mask.5.1 dw.6.1 dw_mask.7.1 dw.6.0 dw_store.5 w1_quant.5 dw.7.0 dw_mask.6.0 dh.2.1 w0_lay.3 dw_mask.7.0 dh.2.0
dz1_mask.2.1 dh.2.2 dz1_mask.2.0 dh.2.3 dz1_mask.2.2 dz1_turn.2.0 dz1_mask.2.3 load_w0.3 w0_quant.3 dz1f_lay.2.0
dz1_turn.2.1 w1_quant.7 dz1t_lay.2 dw_mask.6.1 dh.3.1 w0_quant.2 dw_store.7 dh.3.3 w0_mask.0 dh.3.2 dz1f_lay.2.1
dz1_mask.3.1 w0_lay.1 dz1_mask.3.2 dh.3.0 dz1_mask.3.3 dz1_mask.3.0 dz1_turn.3.1 dz1t_quant.2 dz1_turn.3.0 w0_lay.0
w0_mask.2 dw.10.1 dw.9.1 dw.11.0 dw_mask.11.0 dz1t_lay.3 w0_quant.0 dw.10.0 dw_mask.9.1 dx.6.0 dx.2.0 dw_mask.10.1
dx.6.1 dx.4.0 w0_quant.1 dx.2.1 dx.4.1 dw_mask.10.0 dw.9.0 dw.11.1 dz1f_quant.2 w0_lay.4 dw.8.0 dw_mask.11.1
dw_mask.9.0 dw.8.1 dw_store.11 dw_mask.8.0 w0_mask.3 dz1f_lay.3.1 dz1f_lay.3.0 dx.5.0 w0_lay.5 dx.5.1 dx.7.0 w0_quant.4
dx.7.1 dw_mask.8.1 dx.4.2 dx.6.2 dz1t_quant.3 dw_store.9 dx.2.2 w0_lay.7 dz1f_quant.3 dw.13.1 dw.15.1 w0_quant.5
dw.13.0 dw_mask.13.1 dx.5.2 dx.7.2 dw_mask.15.1 dw.15.0 dw_mask.13.0 w0_lay.6 dw.12.1 dw_mask.15.0 dw.12.0 dw_mask.12.1
dw.14.0 dw_store.15 dw_mask.12.0 dw.14.1 w0_quant.7 dw_store.13 w0_quant.6 dx.5.3 dx.7.3 dw_mask.14.1 dx_copy.5 dx.6.3
dx.2.3 dw_mask.14.0 dx_copy.7 dx.4.3 dx.3.0 dx_copy.6 dw_store.14 dx.1.0 dx.3.1 dx_copy.4 dx_store.3 dx.0.0 dx.3.2
dx_copy.2 dx_store.2 dx.0.1 dx.3.3 dx.0.2 dx_copy.3 dx.1.1 dx.0.3 dx.1.2 dx_store.1 dx_copy.0 dx.1.3 dx_copy.1
dx_store.0
"""


def tile_patchedsparsenetwork_pa_v_kernel(tc, x, W0, b0, m0, W1, b1, m1, pre0, pre1, grad_out, out_0, out_1):
    nc = tc.nc
    with ExitStack() as ctx:
        keep = ctx.enter_context(tc.tile_pool(name="keep", bufs=1))
        work = ctx.enter_context(tc.tile_pool(name="work", bufs=2))
        psum = ctx.enter_context(tc.psum_pool(name="psum", bufs=1))
        ctx.enter_context(tc.manual_schedule())

        identity = keep.tile([P, P], F32, name="identity")
        make_identity(nc, identity[:])

        def quantised(width, name):
            return (keep.tile([P, width], U32, name=name + "_codes", align_bytes=64),
                    keep.tile([P, width], U8, name=name + "_scales", align_bytes=64))

        dz2_q = quantised(G * B, "dz2")
        dz1f_q = quantised(Q * B, "dz1f")
        dz1t_q = quantised(D1, "dz1t")
        x_q = quantised(D0, "x")
        w0_q = quantised(Q * D0, "w0")

        by_token = "(p j) w -> p j w"
        by_pass = "(g p j) w -> g p j w"
        pre1_v, grad_v, pre0_v, x_v, out0_v = (a.rearrange(by_token, j=T) for a in (pre1, grad_out, pre0, x, out_0))
        w1_v, m1_v, w0_v, m0_v, out1_v = (a.rearrange(by_pass, p=P, j=T) for a in (W1, m1, W0, m0, out_1))

        live = {}

        def part(i, width):
            return slice(i * width, (i + 1) * width)

        def kept(key, make):
            if key not in live:
                live[key] = make()
            return live[key]

        def sbuf(tag, shape, dtype, bufs):
            return work.tile(shape, dtype, name=tag, tag=tag, bufs=bufs, align_bytes=64)

        def bank(tag, shape, bufs):
            return psum.tile(shape, F32, name=tag, tag=tag, bufs=bufs)

        def big(shape, dtype=BF16):
            return sbuf("big", shape, dtype, 9)

        def outs():
            return sbuf("outs", [P, 2, D0], F32, 4)

        def grouped():
            return sbuf("grouped", [P, N, T], BF16, 4)

        def turned(tag):
            return bank(tag, [P, 2, 2, P], 2)

        def load_pre1(j):
            rows = kept(("pre1", j // 2), outs)
            nc.sync.dma_start(out=rows[:, j % 2], in_=pre1_v[:, j, :])

        def load_grad(j):
            rows = kept("grad", lambda: big([P, T * D2]))
            nc.sync.dma_start(out=rows[:, part(j, D2)], in_=grad_v[:, j, :])

        def load_half(name, src, h, g):
            live[name, h, g] = sbuf(name + "_2", [P, T, H * N], BF16, 2)
            nc.sync.dma_start(out=live[name, h, g][:], in_=src[g, :, :, part(h, H * N)])

        def load_w1(h, g):
            load_half("w1", w1_v, h, g)

        def load_m1(h, g):
            load_half("m1", m1_v, h, g)

        def load_pre0(q):
            live["pre0", q] = big([P, T, N], F32)
            nc.sync.dma_start(out=live["pre0", q][:], in_=pre0_v[:, :, part(q, N)])

        def load_m0(q):
            live["m0", q] = big([P, T, D0])
            nc.sync.dma_start(out=live["m0", q][:], in_=m0_v[q])

        def load_w0(q):
            live["w0", q] = big([P, T, D0])
            nc.sync.dma_start(out=live["w0", q][:], in_=w0_v[q])

        def load_x():
            live["x"] = big([P, T, D0])
            nc.sync.dma_start(out=live["x"][:], in_=x_v)

        def turn(words, where):
            for u in range(2):
                nc.tensor.transpose(where[:, u, :], words[:, u:2 * P:2], identity[:])

        def lay(rows):
            tile = grouped()
            nc.scalar.copy(out=tile[:].rearrange("p (c i) t -> p c t i", i=4), in_=rows.rearrange("p t (c i) -> p c t i", i=4))
            return tile

        def lay_on_gpsimd(rows):
            tile = grouped()
            nc.gpsimd.tensor_scalar(out=tile[:], in0=rows.rearrange("p t w -> p w t"), scalar1=1.0, scalar2=0.0, op0=MULT, op1=ADD)
            return tile

        def quantise(planes, cols, words, fmt):
            codes, scales = planes
            nc.vector.quantize_mx(out=codes[:, cols].bitcast(fmt), scales=scales[:, cols], in_=words)

        def product(out, left, left_cols, right, right_cols, first, last):
            (lc, ls), (rc, rs) = left, right
            nc.tensor.matmul_mx(out=out[:], lhsT=lc[:, left_cols].bitcast(E5M2X4), lhsT_scale=ls[:, left_cols],
                                rhs=rc[:, right_cols].bitcast(E4M3X4), rhs_scale=rs[:, right_cols], start=first, stop=last)

        def dz2_mask(j):
            live["dz2", j] = sbuf("dz2", [P, D2], BF16, 2)
            nc.vector.scalar_tensor_tensor(out=live["dz2", j][:], in0=live["pre1", j // 2][:, j % 2], scalar=0.0,
                                           in1=live["grad"][:, part(j, D2)], op0=GT, op1=MULT)

        def dz2_turn(j):
            live["dz2_t", j] = turned("turned")
            words = live["dz2", j][:].bitcast(F32)
            for g in range(G):
                turn(words[:, part(g, 2 * P)], live["dz2_t", j][:, g])

        def dz2_lay(j):
            tile = kept("dz2_g", lambda: big([P, G, T, P, T]))
            nc.scalar.copy(out=tile[:, :, j].bitcast(F32), in_=live["dz2_t", j][:].rearrange("p g u m -> p g m u"))

        def dz2_quant(g):
            quantise(dz2_q, part(g, B), live["dz2_g"][:, g].rearrange("p j m t -> p (j m t)"), E5M2X4)

        def w1_mask(h, g):
            w = live["w1", h, g]
            nc.vector.tensor_tensor(out=w[:], in0=w[:], in1=live["m1", h, g][:], op=MULT)

        def w1_lay(k):
            q, g = k // G, k % G
            live["w1_g", k] = lay(live["w1", q // H, g][:, :, part(q % H, N)])

        def w1_quant(k):
            live["w1_q", k] = (sbuf("w1_codes", [P, N], U32, 5), sbuf("w1_scales", [P, N], U8, 5))
            quantise(live["w1_q", k], slice(0, N), live["w1_g", k][:].rearrange("p w t -> p (w t)"), E4M3X4)

        def dh(q, j):
            live["dh", q, j] = bank("dh", [P, N], 3)
            for g in range(G):
                product(live["dh", q, j], dz2_q, slice(g * B + j * P, g * B + (j + 1) * P), live["w1_q", G * q + g], slice(0, N),
                        g == 0, g == G - 1)

        def dz1_mask(q, j):
            tile = kept(("dz1", q), lambda: sbuf("dz1", [P, T, N], BF16, 2))
            nc.vector.scalar_tensor_tensor(out=tile[:, j], in0=live["pre0", q][:, j], scalar=0.0, in1=live["dh", q, j][:],
                                           op0=GT, op1=MULT)

        def dz1_turn(q, pair):
            live["dz1_t", q, pair] = turned("turned")
            for i in range(2):
                turn(live["dz1", q][:, 2 * pair + i].bitcast(F32), live["dz1_t", q, pair][:, i])

        def dz1f_lay(q, pair):
            tile = kept(("dz1f_g", q), lambda: sbuf("dz1f_g", [P, T, P, T], BF16, 1))
            nc.scalar.copy(out=tile[:, part(pair, 2)].bitcast(F32),
                           in_=live["dz1_t", q, pair][:].rearrange("p j u m -> p j m u"))

        def dz1f_quant(q):
            quantise(dz1f_q, part(q, B), live["dz1f_g", q][:].rearrange("p j m t -> p (j m t)"), E5M2X4)

        def dz1t_lay(q):
            live["dz1t_g", q] = sbuf("dz1t_g", [P, T, P, T], BF16, 1)
            nc.scalar.copy(out=live["dz1t_g", q][:].rearrange("p c m t -> p m t c"),
                           in_=live["dz1", q][:].rearrange("p t (m c) -> p m t c", c=T))

        def dz1t_quant(q):
            quantise(dz1t_q, part(q, N), live["dz1t_g", q][:].rearrange("p c m t -> p (c m t)"), E5M2X4)

        def x_lay(n):
            live["x_g", n] = lay_on_gpsimd(live["x"][:, :, part(n, N)])

        def x_quant(n):
            quantise(x_q, part(n, N), live["x_g", n][:].rearrange("p w t -> p (w t)"), E4M3X4)

        def w0_mask(q):
            w = live["w0", q]
            nc.vector.tensor_tensor(out=w[:], in0=w[:], in1=live["m0", q][:], op=MULT)

        def w0_lay(i):
            live["w0_g", i] = lay(live["w0", i // 2][:, :, part(i % 2, N)])

        def w0_quant(i):
            quantise(w0_q, part(i, N), live["w0_g", i][:].rearrange("p w t -> p (w t)"), E4M3X4)

        def dw(i, n):
            live["dw", i, n] = bank("dw", [P, N], 3)
            product(live["dw", i, n], dz1t_q, part(i, P), x_q, part(n, N), True, True)

        def dw_mask(i, n):
            rows = kept(("dw_out", i // 2), outs)
            nc.vector.tensor_tensor(out=rows[:, i % 2, part(n, N)], in0=live["dw", i, n][:],
                                    in1=live["m0", i // T][:, i % T, part(n, N)], op=MULT)

        def dw_store(i):
            q, c = i // T, i % T
            rows = live["dw_out", i // 2]
            if i >= LAST:
                nc.sync.dma_start(out=out1_v[q, :, c, :], in_=rows[:, i % 2])
            else:
                nc.sync.dma_start(out=out1_v[q, :, c - 1:c + 1, :], in_=rows[:])

        def dx(b, q):
            j, n = b // 2, b % 2
            if q == 0:
                live["dx", b] = bank("turned", [P, N], 2) if n else bank("dh", [P, N], 3)
            product(live["dx", b], dz1f_q, slice(q * B + j * P, q * B + (j + 1) * P), w0_q, slice(q * D0 + n * N, q * D0 + (n + 1) * N),
                    q == 0, q == Q - 1)

        def dx_copy(b):
            rows = kept(("dx_out", b // 4), outs)
            nc.scalar.copy(out=rows[:, b // 2 % 2, part(b % 2, N)], in_=live["dx", b][:])

        def dx_store(j):
            nc.sync.dma_start(out=out0_v[:, j, :], in_=live["dx_out", j // 2][:, j % 2])

        steps = {
            "load_pre1": load_pre1, "load_grad": load_grad, "load_w1": load_w1, "load_m1": load_m1, "load_pre0": load_pre0,
            "load_m0": load_m0, "load_w0": load_w0, "load_x": load_x,
            "dz2_mask": dz2_mask, "dz2_turn": dz2_turn, "dz2_lay": dz2_lay, "dz2_quant": dz2_quant,
            "w1_mask": w1_mask, "w1_lay": w1_lay, "w1_quant": w1_quant,
            "dh": dh, "dz1_mask": dz1_mask, "dz1_turn": dz1_turn, "dz1f_lay": dz1f_lay, "dz1f_quant": dz1f_quant,
            "dz1t_lay": dz1t_lay, "dz1t_quant": dz1t_quant,
            "x_lay": x_lay, "x_quant": x_quant, "w0_mask": w0_mask, "w0_lay": w0_lay, "w0_quant": w0_quant,
            "dw": dw, "dw_mask": dw_mask, "dw_store": dw_store, "dx": dx, "dx_copy": dx_copy, "dx_store": dx_store,
        }
        for word in ORDER.split():
            step = word.split(".")
            steps[step[0]](*[int(index) for index in step[1:]])
